import numpy as np
import ml_dtypes


def mxq(x, axis, fmt="e4m3"):
    dtype, down = {"e4m3": (ml_dtypes.float8_e4m3fn, 7), "e5m2": (ml_dtypes.float8_e5m2, 14)}[fmt]
    v = np.moveaxis(np.asarray(x, np.float32).astype(ml_dtypes.bfloat16).astype(np.float64), axis, -1)
    blocks = v.reshape(v.shape[:-1] + (-1, 32))
    amax = np.abs(blocks).max(-1, keepdims=True)
    byte = np.maximum(np.where(amax > 0, np.frexp(amax)[1] - 1 + 127, 0) - down, 1)
    scale = np.exp2(byte - 127.0)
    codes = (blocks / scale).astype(np.float32).astype(dtype).astype(np.float64)
    return np.moveaxis((codes * scale).reshape(v.shape), -1, axis)


WIDE = False


def mx_kscale(k):
    if not WIDE:
        return np.ones(k)
    levels = np.array([10, -10, 5, -5, 0])
    a = np.random.permutation(np.resize(levels, k // 512 * 4)).reshape(k // 512, 4)
    idx = np.arange(k)
    return np.exp2(a[idx // 512, idx % 128 // 32])


BF16 = ml_dtypes.bfloat16


def bf(x):
    return np.asarray(x, np.float32).astype(BF16)


def f64(x):
    return np.asarray(x).astype(np.float64)


E2M1 = np.array([0.0, 0.5, 1.0, 1.5, 2.0, 3.0, 4.0, 6.0, -0.0, -0.5, -1.0, -1.5, -2.0, -3.0, -4.0, -6.0])


def pack_weight(w, fmt):
    k, n = w.shape
    w = f64(bf(w)).reshape(k // 32, 32, n)
    amax = np.abs(w).max(1)
    if fmt == "e4m3":
        byte = np.frexp(amax)[1] - 1 + 127 - 7
    else:
        mant, ex = np.frexp(amax / 6.0)
        byte = np.where(mant > 0.5, ex, ex - 1) + 127
    byte = np.clip(np.where(amax > 0, byte, 1), 1, 254)
    scaled = (w * np.exp2(127.0 - byte)[:, None, :]).reshape(k, n).astype(np.float32)
    by_word = np.ascontiguousarray(scaled.reshape(k // 512, 128, 4, n).transpose(0, 1, 3, 2))
    if fmt == "e4m3":
        words = by_word.astype(ml_dtypes.float8_e4m3fn).view(np.uint8)
    else:
        c = by_word.astype(ml_dtypes.float4_e2m1fn).view(np.uint8) & 0xF
        words = c[..., 0::2] | (c[..., 1::2] << 4)
    return np.ascontiguousarray(words), np.ascontiguousarray(byte.astype(np.uint8).reshape(k // 512, 16, n))


def unpack_weight(words, scales, fmt):
    g, p, n, _ = words.shape
    if fmt == "e4m3":
        vals = np.ascontiguousarray(words).view(ml_dtypes.float8_e4m3fn).astype(np.float64)
    else:
        nib = np.empty((g, p, n, 4), np.uint8)
        nib[..., 0::2] = words & 0xF
        nib[..., 1::2] = words >> 4
        vals = E2M1[nib]
    vals = vals * np.repeat(np.exp2(scales.astype(np.float64) - 127.0), 8, axis=1)[..., None]
    return vals.transpose(0, 1, 3, 2).reshape(g * 512, n)

def pack4(w):
    words, scales = pack_weight(w, "e2m1")
    return words.reshape(words.shape[0], 128, -1), scales


def unpack4(words, scales):
    return unpack_weight(words.reshape(words.shape[0], 128, -1, 2), scales, "e2m1")


N, MI0, MI1, MS, MG, MO0, MO1, DV = 256, 1024, 512, 2048, 1024, 1024, 512, 3
EPS = 1e-5


def irlin_mx(x, mul0, mul1, w0, w1):
    n = x.shape[0]
    x0 = x[:, :mul0]
    x1 = x[:, mul0:].reshape(n, mul1, DV).transpose(0, 2, 1)
    y0 = (mxq(x0, 1, "e4m3") @ w0) * (1.0 / np.sqrt(mul0))
    y1 = (mxq(x1, 2, "e4m3") @ w1).transpose(0, 2, 1) * (1.0 / np.sqrt(mul1))
    return np.concatenate([y0, y1.reshape(n, -1)], axis=-1)


def irlin_plain(x, mul0, mul1, w0, w1):
    n = x.shape[0]
    x0 = x[:, :mul0]
    x1 = x[:, mul0:].reshape(n, mul1, DV).transpose(0, 2, 1)
    y0 = (x0 @ w0) * (1.0 / np.sqrt(mul0))
    y1 = (x1 @ w1).transpose(0, 2, 1) * (1.0 / np.sqrt(mul1))
    return np.concatenate([y0, y1.reshape(n, -1)], axis=-1)


def batchnorm(x, w, b):
    n = x.shape[0]
    s = x[:, :MO0]
    v = x[:, MO0:].reshape(n, MO1, DV)
    s = s - s.mean(0)
    s_inv = 1.0 / np.sqrt((s * s).mean(0) + EPS)
    s = s * (s_inv * w[:MO0]) + b
    v_inv = 1.0 / np.sqrt((v * v).mean(-1).mean(0) + EPS)
    v = v * (v_inv * w[MO0:])[None, :, None]
    return np.concatenate([s, v.reshape(n, -1)], axis=-1)


def setup_inputs():
    s0, s1 = mx_kscale(MS), mx_kscale(MG)
    h0 = (0.1 + 0.3 * np.random.standard_normal((N, MS))) * s0
    h1 = 0.28 * np.random.standard_normal((N, MG, DV)) * s1[None, :, None]
    features = bf(np.random.standard_normal((N, MI0 + DV * MI1)))
    w0_words, w0_scales = pack4(np.random.standard_normal((MS, MO0)) / s0[:, None])
    w1_words, w1_scales = pack4(np.random.standard_normal((MG, MO1)) / s1[:, None])
    return {"h2": bf(np.concatenate([h0, h1.reshape(N, -1)], axis=-1)),
            "features": features,
            "lin3_W0_words": w0_words,
            "lin3_W0_scales": w0_scales,
            "lin3_W1_words": w1_words,
            "lin3_W1_scales": w1_scales,
            "byp_W0": bf(np.random.standard_normal((MI0, MO0))),
            "byp_W1": bf(np.random.standard_normal((MI1, MO1))),
            "bn_weight": bf(1.0 + 0.1 * np.random.standard_normal(MO0 + MO1)),
            "bn_bias": bf(0.1 * np.random.standard_normal(MO0))}


def reference(h2, features, lin3_W0_words, lin3_W0_scales, lin3_W1_words, lin3_W1_scales, byp_W0, byp_W1, bn_weight, bn_bias):
    out = irlin_mx(f64(h2), MS, MG, unpack4(lin3_W0_words, lin3_W0_scales), unpack4(lin3_W1_words, lin3_W1_scales))
    out = out + irlin_plain(f64(features), MI0, MI1, f64(byp_W0), f64(byp_W1))
    return batchnorm(out, f64(bn_weight), f64(bn_bias))

@@ -1,0 +1,398 @@
+from contextlib import ExitStack
+import math
+
+import concourse.mybir as mybir
+from concourse.masks import make_identity
+
+BF16 = mybir.dt.bfloat16
+F32 = mybir.dt.float32
+I32 = mybir.dt.int32
+U8 = mybir.dt.uint8
+U32 = mybir.dt.uint32
+FP8X4 = mybir.dt.float8_e4m3fn_x4
+FP4X4 = mybir.dt.float4_e2m1fn_x4
+ACT = mybir.ActivationFunctionType
+ALU = mybir.AluOpType
+
+P = 128
+NODES = 256
+HALVES = NODES // P
+DV = 3
+K_PASS = 4 * P
+
+S_HID, V_HID = 2048, 1024
+S_BYP, V_BYP = 1024, 512
+S_OUT, V_OUT = 1024, 512
+S_COLS, V_COLS = NODES, DV * NODES
+S_PASSES, V_PASSES = S_HID // K_PASS, V_HID // K_PASS
+S_CHUNKS, V_CHUNKS = S_BYP // (2 * P), V_BYP // (2 * P)
+S_TILES, V_TILES = S_OUT // P, V_OUT // P
+BANK = 512
+GAINS = S_TILES + V_TILES
+EPS = 1e-5
+
+LAG = 2
+TILES_PER_STORE = BANK // P
+
+FLOPS = 2 * NODES * (S_HID * S_OUT + DV * V_HID * V_OUT + S_BYP * S_OUT + DV * V_BYP * V_OUT)
+
+
+def half_rows(h):
+    return slice(P * h, P * (h + 1))
+
+
+def block(b):
+    return slice(P * b, P * (b + 1))
+
+
+def load_scale_rows(nc, planes, scales):
+    by_row = scales.rearrange("g q n -> q g n")
+    for q in range(8):
+        first = 32 * (q // 4) + q % 4
+        nc.sync.dma_start(
+            out=planes[first:P:64].bitcast(I32), in_=by_row[q:16:8].bitcast(I32)
+        )
+
+
+def transpose_four(nc, psum, identity, blocks):
+    bank = psum.tile([P, 4, P], F32, tag="tr")
+    for j in range(4):
+        nc.tensor.transpose(bank[:, j, :], blocks[j], identity[:])
+    return bank
+
+
+def copy_words(nc, turn, out, in_):
+    if turn % 2 == 0:
+        nc.vector.tensor_copy(out=out, in_=in_)
+    else:
+        nc.scalar.copy(out=out, in_=in_)
+
+
+def mx_group(nc, acc, weight, moving, m, cols):
+    passes = weight["passes"]
+    for g in range(passes):
+        nc.tensor.matmul_mx(
+            out=acc,
+            lhsT=weight["words"][:, g, 2 * P * m : 2 * P * (m + 1)].bitcast(FP4X4),
+            lhsT_scale=weight["planes"][:, g, block(m)],
+            rhs=moving["codes"][:, g, cols].bitcast(FP8X4),
+            rhs_scale=moving["planes"][:, g, cols],
+            start=(g == 0),
+            stop=(g == passes - 1),
+        )
+
+
+def bypass_group(nc, acc, weights, moving, m, cols):
+    chunks = weights.shape[1]
+    for c in range(chunks):
+        for e in range(2):
+            nc.tensor.matmul(
+                out=acc,
+                lhsT=weights[:, c, e, block(m)],
+                rhs=moving[:, c, cols, e],
+                start=(c == 0 and e == 0),
+                stop=(c == chunks - 1 and e == 1),
+            )
+
+
+def tile_feedforward_pb_kernel(
+    tc,
+    h2,
+    features,
+    lin3_W0_words,
+    lin3_W0_scales,
+    lin3_W1_words,
+    lin3_W1_scales,
+    byp_W0,
+    byp_W1,
+    bn_weight,
+    bn_bias,
+    out,
+):
+    nc = tc.nc
+    with ExitStack() as stack:
+        keep = stack.enter_context(tc.tile_pool(name="keep", bufs=1))
+        work = stack.enter_context(tc.tile_pool(name="work", bufs=LAG + 2))
+        small = stack.enter_context(tc.tile_pool(name="small", bufs=LAG + 2))
+        psum = stack.enter_context(tc.psum_pool(name="psum", bufs=4))
+
+        h2s = [keep.tile([P, S_HID], BF16, name="h2s%d" % h) for h in range(HALVES)]
+        h2v = [keep.tile([P, DV * V_HID], BF16, name="h2v%d" % h) for h in range(HALVES)]
+        fs = [keep.tile([P, S_BYP], BF16, name="fs%d" % h) for h in range(HALVES)]
+        fv = [keep.tile([P, DV * V_BYP], BF16, name="fv%d" % h) for h in range(HALVES)]
+        w0 = {
+            "words": keep.tile([P, S_PASSES, 2 * S_OUT], U8, name="w0_words", align_bytes=64),
+            "planes": keep.tile([P, S_PASSES, S_OUT], U8, name="w0_planes", align_bytes=64),
+            "passes": S_PASSES,
+        }
+        w1 = {
+            "words": keep.tile([P, V_PASSES, 2 * V_OUT], U8, name="w1_words", align_bytes=64),
+            "planes": keep.tile([P, V_PASSES, V_OUT], U8, name="w1_planes", align_bytes=64),
+            "passes": V_PASSES,
+        }
+        bw0 = keep.tile([P, S_CHUNKS, 2, S_OUT], BF16)
+        bw1 = keep.tile([P, V_CHUNKS, 2, V_OUT], BF16)
+
+        nc.vector.memset(w0["planes"][:].bitcast(I32), 0)
+        nc.vector.memset(w1["planes"][:].bitcast(I32), 0)
+        eps = keep.tile([P, 1], F32)
+        nc.vector.memset(eps[:], EPS)
+        norm_rows = keep.tile([P, P], BF16)
+        nc.vector.memset(norm_rows[:], 0.0)
+        identity = keep.tile([P, P], F32)
+        make_identity(nc, identity[:])
+        warm = keep.tile([P, 1], F32)
+        nc.scalar.activation(out=warm[:], in_=eps[:], func=ACT.Sqrt)
+
+        for h in range(HALVES):
+            nc.sync.dma_start(out=h2s[h][:], in_=h2[half_rows(h), 0:S_HID])
+        load_scale_rows(nc, w0["planes"], lin3_W0_scales)
+        load_scale_rows(nc, w1["planes"], lin3_W1_scales)
+        nc.sync.dma_start(
+            out=w0["words"][:].bitcast(I32),
+            in_=lin3_W0_words.rearrange("g p b -> p g b").bitcast(I32),
+        )
+        for h in range(HALVES):
+            nc.sync.dma_start(out=h2v[h][:], in_=h2[half_rows(h), S_HID:])
+        nc.sync.dma_start(
+            out=w1["words"][:].bitcast(I32),
+            in_=lin3_W1_words.rearrange("g p b -> p g b").bitcast(I32),
+        )
+        for h in range(HALVES):
+            nc.sync.dma_start(out=fv[h][:], in_=features[half_rows(h), S_BYP:])
+        for h in range(HALVES):
+            nc.sync.dma_start(out=fs[h][:], in_=features[half_rows(h), 0:S_BYP])
+        nc.sync.dma_start(out=bw1[:], in_=byp_W1.rearrange("(c q e) o -> q c e o", q=P, e=2))
+        nc.sync.dma_start(out=bw0[:], in_=byp_W0.rearrange("(c q e) o -> q c e o", q=P, e=2))
+        nc.scalar.dma_start(out=norm_rows[0:GAINS, :], in_=bn_weight.rearrange("(r c) -> r c", c=P))
+        nc.scalar.dma_start(
+            out=norm_rows[GAINS : GAINS + S_TILES, :], in_=bn_bias.rearrange("(r c) -> r c", c=P)
+        )
+
+        s_grouped = keep.tile([P, S_PASSES, S_COLS, 4], BF16, align_bytes=64)
+        s_moving = {
+            "codes": keep.tile([P, S_PASSES, S_COLS], U32, name="s_codes", align_bytes=64),
+            "planes": keep.tile([P, S_PASSES, S_COLS], U8, name="s_planes", align_bytes=64),
+        }
+        turn = 0
+        for h in range(HALVES):
+            words = h2s[h][:].bitcast(F32).rearrange("n (g q u) -> n g u q", q=P, u=2)
+            for g0 in range(0, S_PASSES, 2):
+                bank = transpose_four(
+                    nc, psum, identity, [words[:, g0 + i, u, :] for i in range(2) for u in range(2)]
+                )
+                copy_words(
+                    nc,
+                    turn,
+                    out=s_grouped[:].bitcast(F32)[:, g0 : g0 + 2, block(h), :],
+                    in_=bank[:].rearrange("q (g u) n -> q g n u", u=2),
+                )
+                turn += 1
+        for g in range(S_PASSES):
+            nc.vector.quantize_mx(
+                out=s_moving["codes"][:, g, :].bitcast(FP8X4),
+                scales=s_moving["planes"][:, g, :],
+                in_=s_grouped[:, g, :, :].rearrange("q n t -> q (n t)"),
+            )
+
+        norm_rows_f32 = keep.tile([P, P], F32)
+        nc.vector.tensor_copy(out=norm_rows_f32[:], in_=norm_rows[:])
+        norm_bank = psum.tile([P, 4, P], F32, tag="tr")
+        nc.tensor.transpose(norm_bank[:, 0, :], norm_rows_f32[:], identity[:])
+        norm_cols = keep.tile([P, GAINS + S_TILES], F32)
+        nc.vector.tensor_copy(out=norm_cols[:], in_=norm_bank[:, 0, 0 : GAINS + S_TILES])
+
+        v_sorted = [keep.tile([P, DV, 2 * V_PASSES, 2 * P], BF16, name="v_sorted%d" % h) for h in range(HALVES)]
+        for h in range(HALVES):
+            by_part = h2v[h][:].rearrange(
+                "n (g q u e d) -> n d g u q e", g=V_PASSES, q=P, u=2, e=2, d=DV
+            )
+            for d in range(DV):
+                for g in range(V_PASSES):
+                    dst = v_sorted[h][:, d, 2 * g : 2 * g + 2, :].rearrange("n u (q e) -> n u q e", e=2)
+                    if d < 2:
+                        nc.vector.tensor_copy(out=dst, in_=by_part[:, d, g])
+                    else:
+                        nc.scalar.copy(out=dst, in_=by_part[:, d, g])
+
+        s_parked = keep.tile([P, S_TILES, S_COLS], F32)
+        for m0 in range(0, S_TILES, 2):
+            acc = psum.tile([P, 2, S_COLS], F32, tag="acc")
+            for i in range(2):
+                for b in range(HALVES):
+                    mx_group(nc, acc[:, i, block(b)], w0, s_moving, m0 + i, block(b))
+            nc.scalar.activation(
+                out=s_parked[:, m0 : m0 + 2, :], in_=acc[:], func=ACT.Copy, scale=1.0 / math.sqrt(S_HID)
+            )
+
+        v_grouped = keep.tile([P, V_PASSES, V_COLS, 4], BF16, align_bytes=64)
+        v_moving = {
+            "codes": keep.tile([P, V_PASSES, V_COLS], U32, name="v_codes", align_bytes=64),
+            "planes": keep.tile([P, V_PASSES, V_COLS], U8, name="v_planes", align_bytes=64),
+        }
+        for h in range(HALVES):
+            words = v_sorted[h][:].bitcast(F32)
+            for d in range(DV):
+                bank = transpose_four(nc, psum, identity, [words[:, d, j, :] for j in range(4)])
+                copy_words(
+                    nc,
+                    turn,
+                    out=v_grouped[:].bitcast(F32)[:, :, block(DV * h + d), :],
+                    in_=bank[:].rearrange("q (g u) n -> q g n u", u=2),
+                )
+                turn += 1
+        for b in range(V_COLS // P):
+            for g in range(V_PASSES):
+                nc.vector.quantize_mx(
+                    out=v_moving["codes"][:, g, block(b)].bitcast(FP8X4),
+                    scales=v_moving["planes"][:, g, block(b)],
+                    in_=v_grouped[:, g, block(b), :].rearrange("q n t -> q (n t)"),
+                )
+
+        f_sorted = [keep.tile([P, DV, V_BYP], BF16, name="f_sorted%d" % h) for h in range(HALVES)]
+        for h in range(HALVES):
+            nc.vector.tensor_copy(out=f_sorted[h][:], in_=fv[h][:].rearrange("n (i d) -> n d i", d=DV))
+        v_feat = keep.tile([P, V_CHUNKS, 2 * V_COLS], BF16)
+        for d in range(DV):
+            bank = transpose_four(
+                nc,
+                psum,
+                identity,
+                [f_sorted[h][:].bitcast(F32)[:, d, block(c)] for h in range(HALVES) for c in range(V_CHUNKS)],
+            )
+            copy_words(
+                nc,
+                turn,
+                out=v_feat[:].bitcast(F32).rearrange("q c (h d n) -> q c h d n", h=HALVES, d=DV)[:, :, :, d, :],
+                in_=bank[:].rearrange("q (h c) n -> q c h n", c=V_CHUNKS),
+            )
+            turn += 1
+        s_feat = keep.tile([P, S_CHUNKS, 2 * S_COLS], BF16)
+        for h in range(HALVES):
+            bank = transpose_four(
+                nc, psum, identity, [fs[h][:].bitcast(F32)[:, block(c)] for c in range(S_CHUNKS)]
+            )
+            copy_words(nc, turn, out=s_feat[:].bitcast(F32)[:, :, block(h)], in_=bank[:])
+            turn += 1
+        v_feat_cols = v_feat[:].rearrange("q c (n e) -> q c n e", e=2)
+        s_feat_cols = s_feat[:].rearrange("q c (n e) -> q c n e", e=2)
+
+        v_parked = keep.tile([P, V_TILES, V_COLS], F32)
+        for m in range(V_TILES):
+            wide = psum.tile([P, BANK], F32, tag="acc")
+            mx_group(nc, wide[:], w1, v_moving, m, slice(0, BANK))
+            rest = psum.tile([P, V_COLS - BANK], F32, tag="acc")
+            for b in range(BANK // P, V_COLS // P):
+                mx_group(nc, rest[:, P * b - BANK : P * (b + 1) - BANK], w1, v_moving, m, block(b))
+            nc.scalar.activation(
+                out=v_parked[:, m, 0:BANK], in_=wide[:], func=ACT.Copy, scale=1.0 / math.sqrt(V_HID)
+            )
+            nc.scalar.activation(
+                out=v_parked[:, m, BANK:], in_=rest[:], func=ACT.Copy, scale=1.0 / math.sqrt(V_HID)
+            )
+
+        def inverse_deviation(sum_of_squares, count, gain):
+            deviation = small.tile([P, 1], F32)
+            nc.scalar.activation(
+                out=deviation[:], in_=sum_of_squares[:], func=ACT.Sqrt, bias=eps[:], scale=1.0 / count
+            )
+            inverse = small.tile([P, 1], F32)
+            nc.vector.reciprocal(out=inverse[:], in_=deviation[:])
+            factor = small.tile([P, 1], F32)
+            nc.vector.tensor_tensor(out=factor[:], in0=inverse[:], in1=gain, op=ALU.mult)
+            return factor
+
+        def vector_tile(m):
+            wide = psum.tile([P, BANK], F32, tag="acc")
+            bypass_group(nc, wide[:], bw1, v_feat_cols, m, slice(0, BANK))
+            rest = psum.tile([P, V_COLS - BANK], F32, tag="acc")
+            bypass_group(nc, rest[:], bw1, v_feat_cols, m, slice(BANK, V_COLS))
+            y = work.tile([P, V_COLS], F32, tag="y")
+            nc.vector.scalar_tensor_tensor(
+                out=y[:, 0:BANK], in0=wide[:], scalar=1.0 / math.sqrt(V_BYP), in1=v_parked[:, m, 0:BANK],
+                op0=ALU.mult, op1=ALU.add,
+            )
+            nc.vector.scalar_tensor_tensor(
+                out=y[:, BANK:], in0=rest[:], scalar=1.0 / math.sqrt(V_BYP), in1=v_parked[:, m, BANK:],
+                op0=ALU.mult, op1=ALU.add,
+            )
+            squares = work.tile([P, V_COLS], F32, tag="squares")
+            sum_of_squares = small.tile([P, 1], F32)
+            nc.scalar.activation(out=squares[:], in_=y[:], func=ACT.Square, accum_out=sum_of_squares[:])
+            factor = inverse_deviation(sum_of_squares, V_COLS, norm_cols[:, S_TILES + m : S_TILES + m + 1])
+            z = work.tile([P, V_COLS], F32, tag="z")
+            nc.gpsimd.tensor_scalar(
+                out=z[:], in0=y[:], scalar1=factor[:], scalar2=0.0, op0=ALU.mult, op1=ALU.add
+            )
+            return z
+
+        def scalar_tile(m):
+            acc = psum.tile([P, S_COLS], F32, tag="acc")
+            bypass_group(nc, acc[:], bw0, s_feat_cols, m, slice(0, S_COLS))
+            y = work.tile([P, S_COLS], F32, tag="y")
+            total = small.tile([P, 1], F32)
+            nc.vector.scalar_tensor_tensor(
+                out=y[:], in0=acc[:], scalar=1.0 / math.sqrt(S_BYP), in1=s_parked[:, m, :],
+                op0=ALU.mult, op1=ALU.add, accum_out=total[:],
+            )
+            minus_mean = small.tile([P, 1], F32)
+            nc.vector.tensor_scalar(
+                out=minus_mean[:], in0=total[:], scalar1=-1.0 / S_COLS, scalar2=None, op0=ALU.mult
+            )
+            squares = work.tile([P, S_COLS], F32, tag="squares")
+            sum_of_squares = small.tile([P, 1], F32)
+            nc.scalar.activation(
+                out=squares[:], in_=y[:], func=ACT.Square, bias=minus_mean[:], accum_out=sum_of_squares[:]
+            )
+            factor = inverse_deviation(sum_of_squares, S_COLS, norm_cols[:, m : m + 1])
+            shift = small.tile([P, 1], F32)
+            nc.vector.scalar_tensor_tensor(
+                out=shift[:], in0=minus_mean[:], scalar=factor[:], in1=norm_cols[:, GAINS + m : GAINS + m + 1],
+                op0=ALU.mult, op1=ALU.add,
+            )
+            z = work.tile([P, S_COLS], F32, tag="z")
+            nc.gpsimd.tensor_scalar(
+                out=z[:], in0=y[:], scalar1=factor[:], scalar2=shift[:], op0=ALU.mult, op1=ALU.add
+            )
+            return z
+
+        def store_vector_tile(m, z):
+            for h in range(HALVES):
+                bank = psum.tile([P, 4, P], F32, tag="tr")
+                for d in range(DV):
+                    nc.tensor.transpose(bank[:, d, :], z[:, block(DV * h + d)], identity[:])
+                rows = work.tile([P, P, DV], F32, tag="rows")
+                copy_words(nc, h, out=rows[:], in_=bank[:, 0:DV, :].rearrange("n d o -> n o d"))
+                first = S_OUT + DV * P * m
+                nc.sync.dma_start(
+                    out=out[half_rows(h), first : first + DV * P], in_=rows[:].rearrange("n o d -> n (o d)")
+                )
+
+        s_banks = {}
+
+        def store_scalar_tile(m, z):
+            place = m % TILES_PER_STORE
+            for h in range(HALVES):
+                if place == 0:
+                    s_banks[h] = psum.tile([P, TILES_PER_STORE, P], F32, tag="tr", name="s_bank")
+                nc.tensor.transpose(s_banks[h][:, place, :], z[:, block(h)], identity[:])
+            if place == TILES_PER_STORE - 1:
+                for h in range(HALVES):
+                    rows = work.tile([P, TILES_PER_STORE, P], F32, tag="rows")
+                    copy_words(nc, h, out=rows[:], in_=s_banks[h][:])
+                    nc.sync.dma_start(
+                        out=out[half_rows(h), P * (m + 1 - TILES_PER_STORE) : P * (m + 1)],
+                        in_=rows[:].rearrange("n m o -> n (m o)"),
+                    )
+
+        normed = {}
+        for i in range(V_TILES + S_TILES + LAG):
+            if i < V_TILES:
+                normed[i] = vector_tile(i)
+            elif i < V_TILES + S_TILES:
+                normed[i] = scalar_tile(i - V_TILES)
+            j = i - LAG
+            if 0 <= j < V_TILES:
+                store_vector_tile(j, normed[j])
+            elif j >= V_TILES:
+                store_scalar_tile(j - V_TILES, normed[j])

@@ -31,7 +31,7 @@ BANK = 512
 GAINS = S_TILES + V_TILES
 EPS = 1e-5
 
-LAG = 2
+LAG = 3
 TILES_PER_STORE = BANK // P
 
 FLOPS = 2 * NODES * (S_HID * S_OUT + DV * V_HID * V_OUT + S_BYP * S_OUT + DV * V_BYP * V_OUT)
@@ -115,6 +115,7 @@ def tile_feedforward_pb_kernel(
         work = stack.enter_context(tc.tile_pool(name="work", bufs=LAG + 2))
         small = stack.enter_context(tc.tile_pool(name="small", bufs=LAG + 2))
         psum = stack.enter_context(tc.psum_pool(name="psum", bufs=4))
+        stack.enter_context(tc.manual_schedule())
 
         h2s = [keep.tile([P, S_HID], BF16, name="h2s%d" % h) for h in range(HALVES)]
         h2v = [keep.tile([P, DV * V_HID], BF16, name="h2v%d" % h) for h in range(HALVES)]
@@ -147,22 +148,22 @@ def tile_feedforward_pb_kernel(
         for h in range(HALVES):
             nc.sync.dma_start(out=h2s[h][:], in_=h2[half_rows(h), 0:S_HID])
         load_scale_rows(nc, w0["planes"], lin3_W0_scales)
-        load_scale_rows(nc, w1["planes"], lin3_W1_scales)
-        nc.sync.dma_start(
-            out=w0["words"][:].bitcast(I32),
-            in_=lin3_W0_words.rearrange("g p b -> p g b").bitcast(I32),
-        )
+        w0_in = lin3_W0_words.rearrange("g p b -> p g b")
+        for part in range(2):
+            some = slice(S_OUT * part, S_OUT * (part + 1))
+            nc.sync.dma_start(out=w0["words"][:, :, some].bitcast(I32), in_=w0_in[:, :, some].bitcast(I32))
+        for h in range(HALVES):
+            nc.sync.dma_start(out=fv[h][:], in_=features[half_rows(h), S_BYP:])
+        nc.sync.dma_start(out=bw1[:], in_=byp_W1.rearrange("(c q e) o -> q c e o", q=P, e=2))
+        for h in range(HALVES):
+            nc.sync.dma_start(out=fs[h][:], in_=features[half_rows(h), 0:S_BYP])
         for h in range(HALVES):
             nc.sync.dma_start(out=h2v[h][:], in_=h2[half_rows(h), S_HID:])
+        load_scale_rows(nc, w1["planes"], lin3_W1_scales)
         nc.sync.dma_start(
             out=w1["words"][:].bitcast(I32),
             in_=lin3_W1_words.rearrange("g p b -> p g b").bitcast(I32),
         )
-        for h in range(HALVES):
-            nc.sync.dma_start(out=fv[h][:], in_=features[half_rows(h), S_BYP:])
-        for h in range(HALVES):
-            nc.sync.dma_start(out=fs[h][:], in_=features[half_rows(h), 0:S_BYP])
-        nc.sync.dma_start(out=bw1[:], in_=byp_W1.rearrange("(c q e) o -> q c e o", q=P, e=2))
         nc.sync.dma_start(out=bw0[:], in_=byp_W0.rearrange("(c q e) o -> q c e o", q=P, e=2))
         nc.scalar.dma_start(out=norm_rows[0:GAINS, :], in_=bn_weight.rearrange("(r c) -> r c", c=P))
         nc.scalar.dma_start(
@@ -174,7 +175,6 @@ def tile_feedforward_pb_kernel(
             "codes": keep.tile([P, S_PASSES, S_COLS], U32, name="s_codes", align_bytes=64),
             "planes": keep.tile([P, S_PASSES, S_COLS], U8, name="s_planes", align_bytes=64),
         }
-        turn = 0
         for h in range(HALVES):
             words = h2s[h][:].bitcast(F32).rearrange("n (g q u) -> n g u q", q=P, u=2)
             for g0 in range(0, S_PASSES, 2):
@@ -183,11 +183,10 @@ def tile_feedforward_pb_kernel(
                 )
                 copy_words(
                     nc,
-                    turn,
+                    g0 // 2,
                     out=s_grouped[:].bitcast(F32)[:, g0 : g0 + 2, block(h), :],
                     in_=bank[:].rearrange("q (g u) n -> q g n u", u=2),
                 )
-                turn += 1
         for g in range(S_PASSES):
             nc.vector.quantize_mx(
                 out=s_moving["codes"][:, g, :].bitcast(FP8X4),
@@ -202,19 +201,6 @@ def tile_feedforward_pb_kernel(
         norm_cols = keep.tile([P, GAINS + S_TILES], F32)
         nc.vector.tensor_copy(out=norm_cols[:], in_=norm_bank[:, 0, 0 : GAINS + S_TILES])
 
-        v_sorted = [keep.tile([P, DV, 2 * V_PASSES, 2 * P], BF16, name="v_sorted%d" % h) for h in range(HALVES)]
-        for h in range(HALVES):
-            by_part = h2v[h][:].rearrange(
-                "n (g q u e d) -> n d g u q e", g=V_PASSES, q=P, u=2, e=2, d=DV
-            )
-            for d in range(DV):
-                for g in range(V_PASSES):
-                    dst = v_sorted[h][:, d, 2 * g : 2 * g + 2, :].rearrange("n u (q e) -> n u q e", e=2)
-                    if d < 2:
-                        nc.vector.tensor_copy(out=dst, in_=by_part[:, d, g])
-                    else:
-                        nc.scalar.copy(out=dst, in_=by_part[:, d, g])
-
         s_parked = keep.tile([P, S_TILES, S_COLS], F32)
         for m0 in range(0, S_TILES, 2):
             acc = psum.tile([P, 2, S_COLS], F32, tag="acc")
@@ -224,30 +210,6 @@ def tile_feedforward_pb_kernel(
             nc.scalar.activation(
                 out=s_parked[:, m0 : m0 + 2, :], in_=acc[:], func=ACT.Copy, scale=1.0 / math.sqrt(S_HID)
             )
-
-        v_grouped = keep.tile([P, V_PASSES, V_COLS, 4], BF16, align_bytes=64)
-        v_moving = {
-            "codes": keep.tile([P, V_PASSES, V_COLS], U32, name="v_codes", align_bytes=64),
-            "planes": keep.tile([P, V_PASSES, V_COLS], U8, name="v_planes", align_bytes=64),
-        }
-        for h in range(HALVES):
-            words = v_sorted[h][:].bitcast(F32)
-            for d in range(DV):
-                bank = transpose_four(nc, psum, identity, [words[:, d, j, :] for j in range(4)])
-                copy_words(
-                    nc,
-                    turn,
-                    out=v_grouped[:].bitcast(F32)[:, :, block(DV * h + d), :],
-                    in_=bank[:].rearrange("q (g u) n -> q g n u", u=2),
-                )
-                turn += 1
-        for b in range(V_COLS // P):
-            for g in range(V_PASSES):
-                nc.vector.quantize_mx(
-                    out=v_moving["codes"][:, g, block(b)].bitcast(FP8X4),
-                    scales=v_moving["planes"][:, g, block(b)],
-                    in_=v_grouped[:, g, block(b), :].rearrange("q n t -> q (n t)"),
-                )
 
         f_sorted = [keep.tile([P, DV, V_BYP], BF16, name="f_sorted%d" % h) for h in range(HALVES)]
         for h in range(HALVES):
@@ -262,71 +224,101 @@ def tile_feedforward_pb_kernel(
             )
             copy_words(
                 nc,
-                turn,
+                d,
                 out=v_feat[:].bitcast(F32).rearrange("q c (h d n) -> q c h d n", h=HALVES, d=DV)[:, :, :, d, :],
                 in_=bank[:].rearrange("q (h c) n -> q c h n", c=V_CHUNKS),
             )
-            turn += 1
         s_feat = keep.tile([P, S_CHUNKS, 2 * S_COLS], BF16)
         for h in range(HALVES):
             bank = transpose_four(
                 nc, psum, identity, [fs[h][:].bitcast(F32)[:, block(c)] for c in range(S_CHUNKS)]
             )
-            copy_words(nc, turn, out=s_feat[:].bitcast(F32)[:, :, block(h)], in_=bank[:])
-            turn += 1
+            copy_words(nc, h + 1, out=s_feat[:].bitcast(F32)[:, :, block(h)], in_=bank[:])
         v_feat_cols = v_feat[:].rearrange("q c (n e) -> q c n e", e=2)
         s_feat_cols = s_feat[:].rearrange("q c (n e) -> q c n e", e=2)
 
+        v_sorted = [keep.tile([P, DV, 2 * V_PASSES, 2 * P], BF16, name="v_sorted%d" % h) for h in range(HALVES)]
+        for h in range(HALVES):
+            by_part = h2v[h][:].rearrange(
+                "n (g q u e d) -> n d g u q e", g=V_PASSES, q=P, u=2, e=2, d=DV
+            )
+            for d in range(DV):
+                for g in range(V_PASSES):
+                    dst = v_sorted[h][:, d, 2 * g : 2 * g + 2, :].rearrange("n u (q e) -> n u q e", e=2)
+                    if d < 2:
+                        nc.vector.tensor_copy(out=dst, in_=by_part[:, d, g])
+                    else:
+                        nc.scalar.copy(out=dst, in_=by_part[:, d, g])
+
+        v_grouped = keep.tile([P, V_PASSES, V_COLS, 4], BF16, align_bytes=64)
+        v_moving = {
+            "codes": keep.tile([P, V_PASSES, V_COLS], U32, name="v_codes", align_bytes=64),
+            "planes": keep.tile([P, V_PASSES, V_COLS], U8, name="v_planes", align_bytes=64),
+        }
+
+        def transpose_h2_vectors(h):
+            words = v_sorted[h][:].bitcast(F32)
+            for d in range(DV):
+                bank = transpose_four(nc, psum, identity, [words[:, d, j, :] for j in range(4)])
+                copy_words(
+                    nc,
+                    d,
+                    out=v_grouped[:].bitcast(F32)[:, :, block(DV * h + d), :],
+                    in_=bank[:].rearrange("q (g u) n -> q g n u", u=2),
+                )
+
+        def quantise_h2_vectors(h):
+            for d in range(DV):
+                for g in range(V_PASSES):
+                    cols = block(DV * h + d)
+                    nc.vector.quantize_mx(
+                        out=v_moving["codes"][:, g, cols].bitcast(FP8X4),
+                        scales=v_moving["planes"][:, g, cols],
+                        in_=v_grouped[:, g, cols, :].rearrange("q n t -> q (n t)"),
+                    )
+
         v_parked = keep.tile([P, V_TILES, V_COLS], F32)
         for m in range(V_TILES):
+            wide = psum.tile([P, BANK], F32, tag="acc")
+            bypass_group(nc, wide[:], bw1, v_feat_cols, m, slice(0, BANK))
+            rest = psum.tile([P, V_COLS - BANK], F32, tag="acc")
+            bypass_group(nc, rest[:], bw1, v_feat_cols, m, slice(BANK, V_COLS))
+            nc.scalar.activation(
+                out=v_parked[:, m, 0:BANK], in_=wide[:], func=ACT.Copy, scale=1.0 / math.sqrt(V_BYP)
+            )
+            nc.scalar.activation(
+                out=v_parked[:, m, BANK:], in_=rest[:], func=ACT.Copy, scale=1.0 / math.sqrt(V_BYP)
+            )
+            if 1 <= m <= HALVES:
+                transpose_h2_vectors(m - 1)
+            if 2 <= m <= HALVES + 1:
+                quantise_h2_vectors(m - 2)
+
+        def start_vector_tile(m):
             wide = psum.tile([P, BANK], F32, tag="acc")
             mx_group(nc, wide[:], w1, v_moving, m, slice(0, BANK))
             rest = psum.tile([P, V_COLS - BANK], F32, tag="acc")
             for b in range(BANK // P, V_COLS // P):
                 mx_group(nc, rest[:, P * b - BANK : P * (b + 1) - BANK], w1, v_moving, m, block(b))
-            nc.scalar.activation(
-                out=v_parked[:, m, 0:BANK], in_=wide[:], func=ACT.Copy, scale=1.0 / math.sqrt(V_HID)
-            )
-            nc.scalar.activation(
-                out=v_parked[:, m, BANK:], in_=rest[:], func=ACT.Copy, scale=1.0 / math.sqrt(V_HID)
-            )
-
-        def inverse_deviation(sum_of_squares, count, gain):
-            deviation = small.tile([P, 1], F32)
-            nc.scalar.activation(
-                out=deviation[:], in_=sum_of_squares[:], func=ACT.Sqrt, bias=eps[:], scale=1.0 / count
-            )
-            inverse = small.tile([P, 1], F32)
-            nc.vector.reciprocal(out=inverse[:], in_=deviation[:])
-            factor = small.tile([P, 1], F32)
-            nc.vector.tensor_tensor(out=factor[:], in0=inverse[:], in1=gain, op=ALU.mult)
-            return factor
-
-        def vector_tile(m):
-            wide = psum.tile([P, BANK], F32, tag="acc")
-            bypass_group(nc, wide[:], bw1, v_feat_cols, m, slice(0, BANK))
-            rest = psum.tile([P, V_COLS - BANK], F32, tag="acc")
-            bypass_group(nc, rest[:], bw1, v_feat_cols, m, slice(BANK, V_COLS))
             y = work.tile([P, V_COLS], F32, tag="y")
             nc.vector.scalar_tensor_tensor(
-                out=y[:, 0:BANK], in0=wide[:], scalar=1.0 / math.sqrt(V_BYP), in1=v_parked[:, m, 0:BANK],
+                out=y[:, 0:BANK], in0=wide[:], scalar=1.0 / math.sqrt(V_HID), in1=v_parked[:, m, 0:BANK],
                 op0=ALU.mult, op1=ALU.add,
             )
             nc.vector.scalar_tensor_tensor(
-                out=y[:, BANK:], in0=rest[:], scalar=1.0 / math.sqrt(V_BYP), in1=v_parked[:, m, BANK:],
+                out=y[:, BANK:], in0=rest[:], scalar=1.0 / math.sqrt(V_HID), in1=v_parked[:, m, BANK:],
                 op0=ALU.mult, op1=ALU.add,
             )
             squares = work.tile([P, V_COLS], F32, tag="squares")
             sum_of_squares = small.tile([P, 1], F32)
             nc.scalar.activation(out=squares[:], in_=y[:], func=ACT.Square, accum_out=sum_of_squares[:])
-            factor = inverse_deviation(sum_of_squares, V_COLS, norm_cols[:, S_TILES + m : S_TILES + m + 1])
-            z = work.tile([P, V_COLS], F32, tag="z")
-            nc.gpsimd.tensor_scalar(
-                out=z[:], in0=y[:], scalar1=factor[:], scalar2=0.0, op0=ALU.mult, op1=ALU.add
+            deviation = small.tile([P, 1], F32)
+            nc.scalar.activation(
+                out=deviation[:], in_=sum_of_squares[:], func=ACT.Sqrt, bias=eps[:], scale=1.0 / V_COLS
             )
-            return z
+            return {"y": y, "deviation": deviation}
 
-        def scalar_tile(m):
+        def start_scalar_tile(m):
             acc = psum.tile([P, S_COLS], F32, tag="acc")
             bypass_group(nc, acc[:], bw0, s_feat_cols, m, slice(0, S_COLS))
             y = work.tile([P, S_COLS], F32, tag="y")
@@ -344,15 +336,37 @@ def tile_feedforward_pb_kernel(
             nc.scalar.activation(
                 out=squares[:], in_=y[:], func=ACT.Square, bias=minus_mean[:], accum_out=sum_of_squares[:]
             )
-            factor = inverse_deviation(sum_of_squares, S_COLS, norm_cols[:, m : m + 1])
+            deviation = small.tile([P, 1], F32)
+            nc.scalar.activation(
+                out=deviation[:], in_=sum_of_squares[:], func=ACT.Sqrt, bias=eps[:], scale=1.0 / S_COLS
+            )
+            return {"y": y, "deviation": deviation, "minus_mean": minus_mean}
+
+        def gain_over_deviation(started, t):
+            inverse = small.tile([P, 1], F32)
+            nc.vector.reciprocal(out=inverse[:], in_=started["deviation"][:])
+            factor = small.tile([P, 1], F32)
+            nc.vector.tensor_tensor(out=factor[:], in0=inverse[:], in1=norm_cols[:, t : t + 1], op=ALU.mult)
+            return factor
+
+        def norm_vector_tile(m, started):
+            factor = gain_over_deviation(started, S_TILES + m)
+            z = work.tile([P, V_COLS], F32, tag="z")
+            nc.gpsimd.tensor_scalar(
+                out=z[:], in0=started["y"][:], scalar1=factor[:], scalar2=0.0, op0=ALU.mult, op1=ALU.add
+            )
+            return z
+
+        def norm_scalar_tile(m, started):
+            factor = gain_over_deviation(started, m)
             shift = small.tile([P, 1], F32)
             nc.vector.scalar_tensor_tensor(
-                out=shift[:], in0=minus_mean[:], scalar=factor[:], in1=norm_cols[:, GAINS + m : GAINS + m + 1],
-                op0=ALU.mult, op1=ALU.add,
+                out=shift[:], in0=started["minus_mean"][:], scalar=factor[:],
+                in1=norm_cols[:, GAINS + m : GAINS + m + 1], op0=ALU.mult, op1=ALU.add,
             )
             z = work.tile([P, S_COLS], F32, tag="z")
-            nc.gpsimd.tensor_scalar(
-                out=z[:], in0=y[:], scalar1=factor[:], scalar2=shift[:], op0=ALU.mult, op1=ALU.add
+            nc.vector.tensor_scalar(
+                out=z[:], in0=started["y"][:], scalar1=factor[:], scalar2=shift[:], op0=ALU.mult, op1=ALU.add
             )
             return z
 
@@ -362,7 +376,7 @@ def tile_feedforward_pb_kernel(
                 for d in range(DV):
                     nc.tensor.transpose(bank[:, d, :], z[:, block(DV * h + d)], identity[:])
                 rows = work.tile([P, P, DV], F32, tag="rows")
-                copy_words(nc, h, out=rows[:], in_=bank[:, 0:DV, :].rearrange("n d o -> n o d"))
+                nc.scalar.copy(out=rows[:], in_=bank[:, 0:DV, :].rearrange("n d o -> n o d"))
                 first = S_OUT + DV * P * m
                 nc.sync.dma_start(
                     out=out[half_rows(h), first : first + DV * P], in_=rows[:].rearrange("n o d -> n (o d)")
@@ -385,12 +399,19 @@ def tile_feedforward_pb_kernel(
                         in_=rows[:].rearrange("n m o -> n (m o)"),
                     )
 
+        tiles = V_TILES + S_TILES
+        started = {}
         normed = {}
-        for i in range(V_TILES + S_TILES + LAG):
+        for i in range(tiles + LAG):
             if i < V_TILES:
-                normed[i] = vector_tile(i)
-            elif i < V_TILES + S_TILES:
-                normed[i] = scalar_tile(i - V_TILES)
+                started[i] = start_vector_tile(i)
+            elif i < tiles:
+                started[i] = start_scalar_tile(i - V_TILES)
+            j = i - 1
+            if 0 <= j < V_TILES:
+                normed[j] = norm_vector_tile(j, started[j])
+            elif V_TILES <= j < tiles:
+                normed[j] = norm_scalar_tile(j - V_TILES, started[j])
             j = i - LAG
             if 0 <= j < V_TILES:
                 store_vector_tile(j, normed[j])

@@ -32,7 +32,6 @@ GAINS = S_TILES + V_TILES
 EPS = 1e-5
 
 LAG = 3
-TILES_PER_STORE = BANK // P
 
 FLOPS = 2 * NODES * (S_HID * S_OUT + DV * V_HID * V_OUT + S_BYP * S_OUT + DV * V_BYP * V_OUT)
 
@@ -145,6 +144,11 @@ def tile_feedforward_pb_kernel(
         warm = keep.tile([P, 1], F32)
         nc.scalar.activation(out=warm[:], in_=eps[:], func=ACT.Sqrt)
 
+        nc.scalar.dma_start(out=norm_rows[0:GAINS, :], in_=bn_weight.rearrange("(r c) -> r c", c=P))
+        nc.scalar.dma_start(
+            out=norm_rows[GAINS : GAINS + S_TILES, :], in_=bn_bias.rearrange("(r c) -> r c", c=P)
+        )
+
         for h in range(HALVES):
             nc.sync.dma_start(out=h2s[h][:], in_=h2[half_rows(h), 0:S_HID])
         load_scale_rows(nc, w0["planes"], lin3_W0_scales)
@@ -165,10 +169,6 @@ def tile_feedforward_pb_kernel(
             in_=lin3_W1_words.rearrange("g p b -> p g b").bitcast(I32),
         )
         nc.sync.dma_start(out=bw0[:], in_=byp_W0.rearrange("(c q e) o -> q c e o", q=P, e=2))
-        nc.scalar.dma_start(out=norm_rows[0:GAINS, :], in_=bn_weight.rearrange("(r c) -> r c", c=P))
-        nc.scalar.dma_start(
-            out=norm_rows[GAINS : GAINS + S_TILES, :], in_=bn_bias.rearrange("(r c) -> r c", c=P)
-        )
 
         s_grouped = keep.tile([P, S_PASSES, S_COLS, 4], BF16, align_bytes=64)
         s_moving = {
@@ -196,10 +196,6 @@ def tile_feedforward_pb_kernel(
 
         norm_rows_f32 = keep.tile([P, P], F32)
         nc.vector.tensor_copy(out=norm_rows_f32[:], in_=norm_rows[:])
-        norm_bank = psum.tile([P, 4, P], F32, tag="tr")
-        nc.tensor.transpose(norm_bank[:, 0, :], norm_rows_f32[:], identity[:])
-        norm_cols = keep.tile([P, GAINS + S_TILES], F32)
-        nc.vector.tensor_copy(out=norm_cols[:], in_=norm_bank[:, 0, 0 : GAINS + S_TILES])
 
         s_parked = keep.tile([P, S_TILES, S_COLS], F32)
         for m0 in range(0, S_TILES, 2):
@@ -236,6 +232,11 @@ def tile_feedforward_pb_kernel(
             copy_words(nc, h + 1, out=s_feat[:].bitcast(F32)[:, :, block(h)], in_=bank[:])
         v_feat_cols = v_feat[:].rearrange("q c (n e) -> q c n e", e=2)
         s_feat_cols = s_feat[:].rearrange("q c (n e) -> q c n e", e=2)
+
+        norm_bank = psum.tile([P, 4, P], F32, tag="tr")
+        nc.tensor.transpose(norm_bank[:, 0, :], norm_rows_f32[:], identity[:])
+        norm_cols = keep.tile([P, GAINS + S_TILES], F32)
+        nc.vector.tensor_copy(out=norm_cols[:], in_=norm_bank[:, 0, 0 : GAINS + S_TILES])
 
         v_sorted = [keep.tile([P, DV, 2 * V_PASSES, 2 * P], BF16, name="v_sorted%d" % h) for h in range(HALVES)]
         for h in range(HALVES):
@@ -365,7 +366,7 @@ def tile_feedforward_pb_kernel(
                 in1=norm_cols[:, GAINS + m : GAINS + m + 1], op0=ALU.mult, op1=ALU.add,
             )
             z = work.tile([P, S_COLS], F32, tag="z")
-            nc.vector.tensor_scalar(
+            nc.gpsimd.tensor_scalar(
                 out=z[:], in0=started["y"][:], scalar1=factor[:], scalar2=shift[:], op0=ALU.mult, op1=ALU.add
             )
             return z
@@ -376,44 +377,45 @@ def tile_feedforward_pb_kernel(
                 for d in range(DV):
                     nc.tensor.transpose(bank[:, d, :], z[:, block(DV * h + d)], identity[:])
                 rows = work.tile([P, P, DV], F32, tag="rows")
-                nc.scalar.copy(out=rows[:], in_=bank[:, 0:DV, :].rearrange("n d o -> n o d"))
+                copy_words(nc, h, out=rows[:], in_=bank[:, 0:DV, :].rearrange("n d o -> n o d"))
                 first = S_OUT + DV * P * m
                 nc.sync.dma_start(
                     out=out[half_rows(h), first : first + DV * P], in_=rows[:].rearrange("n o d -> n (o d)")
                 )
 
-        s_banks = {}
+        s_bank = {}
 
         def store_scalar_tile(m, z):
-            place = m % TILES_PER_STORE
+            place = m % 2
+            if place == 0:
+                s_bank[0] = psum.tile([P, HALVES, 2, P], F32, tag="tr", name="pair_bank")
             for h in range(HALVES):
-                if place == 0:
-                    s_banks[h] = psum.tile([P, TILES_PER_STORE, P], F32, tag="tr", name="s_bank")
-                nc.tensor.transpose(s_banks[h][:, place, :], z[:, block(h)], identity[:])
-            if place == TILES_PER_STORE - 1:
-                for h in range(HALVES):
-                    rows = work.tile([P, TILES_PER_STORE, P], F32, tag="rows")
-                    copy_words(nc, h, out=rows[:], in_=s_banks[h][:])
-                    nc.sync.dma_start(
-                        out=out[half_rows(h), P * (m + 1 - TILES_PER_STORE) : P * (m + 1)],
-                        in_=rows[:].rearrange("n m o -> n (m o)"),
-                    )
+                nc.tensor.transpose(s_bank[0][:, h, place, :], z[:, block(h)], identity[:])
+            if place == 1:
+                rows = work.tile([P, HALVES, 2, P], F32, tag="rows")
+                nc.scalar.copy(out=rows[:], in_=s_bank[0][:])
+                nc.sync.dma_start(
+                    out=out.rearrange("(h n) c -> n h c", n=P)[:, :, P * (m - 1) : P * (m + 1)],
+                    in_=rows[:].rearrange("n h m o -> n h (m o)"),
+                )
 
-        tiles = V_TILES + S_TILES
+        order = []
+        for m in range(V_TILES):
+            order.extend([("v", m), ("s", 2 * m), ("s", 2 * m + 1)])
         started = {}
         normed = {}
-        for i in range(tiles + LAG):
-            if i < V_TILES:
-                started[i] = start_vector_tile(i)
-            elif i < tiles:
-                started[i] = start_scalar_tile(i - V_TILES)
+        for i in range(len(order) + LAG):
+            if i < len(order):
+                kind, m = order[i]
+                started[i] = start_vector_tile(m) if kind == "v" else start_scalar_tile(m)
             j = i - 1
-            if 0 <= j < V_TILES:
-                normed[j] = norm_vector_tile(j, started[j])
-            elif V_TILES <= j < tiles:
-                normed[j] = norm_scalar_tile(j - V_TILES, started[j])
+            if 0 <= j < len(order):
+                kind, m = order[j]
+                normed[j] = norm_vector_tile(m, started[j]) if kind == "v" else norm_scalar_tile(m, started[j])
             j = i - LAG
-            if 0 <= j < V_TILES:
-                store_vector_tile(j, normed[j])
-            elif j >= V_TILES:
-                store_scalar_tile(j - V_TILES, normed[j])
+            if j >= 0:
+                kind, m = order[j]
+                if kind == "v":
+                    store_vector_tile(m, normed[j])
+                else:
+                    store_scalar_tile(m, normed[j])

@@ -46,11 +46,8 @@ def block(b):
 
 def load_scale_rows(nc, planes, scales):
     by_row = scales.rearrange("g q n -> q g n")
-    for q in range(8):
-        first = 32 * (q // 4) + q % 4
-        nc.sync.dma_start(
-            out=planes[first:P:64].bitcast(I32), in_=by_row[q:16:8].bitcast(I32)
-        )
+    for r in range(4):
+        nc.sync.dma_start(out=planes[r:P:32].bitcast(I32), in_=by_row[r:16:4].bitcast(I32))
 
 
 def transpose_four(nc, psum, identity, blocks):
@@ -144,11 +141,6 @@ def tile_feedforward_pb_kernel(
         warm = keep.tile([P, 1], F32)
         nc.scalar.activation(out=warm[:], in_=eps[:], func=ACT.Sqrt)
 
-        nc.scalar.dma_start(out=norm_rows[0:GAINS, :], in_=bn_weight.rearrange("(r c) -> r c", c=P))
-        nc.scalar.dma_start(
-            out=norm_rows[GAINS : GAINS + S_TILES, :], in_=bn_bias.rearrange("(r c) -> r c", c=P)
-        )
-
         for h in range(HALVES):
             nc.sync.dma_start(out=h2s[h][:], in_=h2[half_rows(h), 0:S_HID])
         load_scale_rows(nc, w0["planes"], lin3_W0_scales)
@@ -156,6 +148,10 @@ def tile_feedforward_pb_kernel(
         for part in range(2):
             some = slice(S_OUT * part, S_OUT * (part + 1))
             nc.sync.dma_start(out=w0["words"][:, :, some].bitcast(I32), in_=w0_in[:, :, some].bitcast(I32))
+        nc.scalar.dma_start(out=norm_rows[0:GAINS, :], in_=bn_weight.rearrange("(r c) -> r c", c=P))
+        nc.scalar.dma_start(
+            out=norm_rows[GAINS : GAINS + S_TILES, :], in_=bn_bias.rearrange("(r c) -> r c", c=P)
+        )
         for h in range(HALVES):
             nc.sync.dma_start(out=fv[h][:], in_=features[half_rows(h), S_BYP:])
         nc.sync.dma_start(out=bw1[:], in_=byp_W1.rearrange("(c q e) o -> q c e o", q=P, e=2))
@@ -187,24 +183,25 @@ def tile_feedforward_pb_kernel(
                     out=s_grouped[:].bitcast(F32)[:, g0 : g0 + 2, block(h), :],
                     in_=bank[:].rearrange("q (g u) n -> q g n u", u=2),
                 )
-        for g in range(S_PASSES):
-            nc.vector.quantize_mx(
-                out=s_moving["codes"][:, g, :].bitcast(FP8X4),
-                scales=s_moving["planes"][:, g, :],
-                in_=s_grouped[:, g, :, :].rearrange("q n t -> q (n t)"),
-            )
+            for g in range(S_PASSES):
+                nc.vector.quantize_mx(
+                    out=s_moving["codes"][:, g, block(h)].bitcast(FP8X4),
+                    scales=s_moving["planes"][:, g, block(h)],
+                    in_=s_grouped[:, g, block(h), :].rearrange("q n t -> q (n t)"),
+                )
 
         norm_rows_f32 = keep.tile([P, P], F32)
         nc.vector.tensor_copy(out=norm_rows_f32[:], in_=norm_rows[:])
 
         s_parked = keep.tile([P, S_TILES, S_COLS], F32)
-        for m0 in range(0, S_TILES, 2):
-            acc = psum.tile([P, 2, S_COLS], F32, tag="acc")
-            for i in range(2):
-                for b in range(HALVES):
-                    mx_group(nc, acc[:, i, block(b)], w0, s_moving, m0 + i, block(b))
+        s_acc = [psum.tile([P, 2, S_COLS], F32, tag="acc", name="s_acc") for pair in range(S_TILES // 2)]
+        for h in range(HALVES):
+            for m in range(S_TILES):
+                mx_group(nc, s_acc[m // 2][:, m % 2, block(h)], w0, s_moving, m, block(h))
+        for pair in range(S_TILES // 2):
             nc.scalar.activation(
-                out=s_parked[:, m0 : m0 + 2, :], in_=acc[:], func=ACT.Copy, scale=1.0 / math.sqrt(S_HID)
+                out=s_parked[:, 2 * pair : 2 * pair + 2, :], in_=s_acc[pair][:], func=ACT.Copy,
+                scale=1.0 / math.sqrt(S_HID),
             )
 
         f_sorted = [keep.tile([P, DV, V_BYP], BF16, name="f_sorted%d" % h) for h in range(HALVES)]

@@ -31,7 +31,7 @@ BANK = 512
 GAINS = S_TILES + V_TILES
 EPS = 1e-5
 
-LAG = 3
+WORK_BUFS = 6
 
 FLOPS = 2 * NODES * (S_HID * S_OUT + DV * V_HID * V_OUT + S_BYP * S_OUT + DV * V_BYP * V_OUT)
 
@@ -108,8 +108,8 @@ def tile_feedforward_pb_kernel(
     nc = tc.nc
     with ExitStack() as stack:
         keep = stack.enter_context(tc.tile_pool(name="keep", bufs=1))
-        work = stack.enter_context(tc.tile_pool(name="work", bufs=LAG + 2))
-        small = stack.enter_context(tc.tile_pool(name="small", bufs=LAG + 2))
+        work = stack.enter_context(tc.tile_pool(name="work", bufs=WORK_BUFS))
+        small = stack.enter_context(tc.tile_pool(name="small", bufs=WORK_BUFS))
         psum = stack.enter_context(tc.psum_pool(name="psum", bufs=4))
         stack.enter_context(tc.manual_schedule())
 
@@ -139,7 +139,7 @@ def tile_feedforward_pb_kernel(
         identity = keep.tile([P, P], F32)
         make_identity(nc, identity[:])
         warm = keep.tile([P, 1], F32)
-        nc.scalar.activation(out=warm[:], in_=eps[:], func=ACT.Sqrt)
+        nc.scalar.activation(out=warm[:], in_=eps[:], func=ACT.Abs_reciprocal_sqrt)
 
         for h in range(HALVES):
             nc.sync.dma_start(out=h2s[h][:], in_=h2[half_rows(h), 0:S_HID])
@@ -292,7 +292,22 @@ def tile_feedforward_pb_kernel(
             if 2 <= m <= HALVES + 1:
                 quantise_h2_vectors(m - 2)
 
-        def start_vector_tile(m):
+        def scalar_product(m):
+            acc = psum.tile([P, S_COLS], F32, tag="acc")
+            bypass_group(nc, acc[:], bw0, s_feat_cols, m, slice(0, S_COLS))
+            y = work.tile([P, S_COLS], F32, tag="y")
+            total = small.tile([P, 1], F32)
+            nc.vector.scalar_tensor_tensor(
+                out=y[:], in0=acc[:], scalar=1.0 / math.sqrt(S_BYP), in1=s_parked[:, m, :],
+                op0=ALU.mult, op1=ALU.add, accum_out=total[:],
+            )
+            minus_mean = small.tile([P, 1], F32)
+            nc.vector.tensor_scalar(
+                out=minus_mean[:], in0=total[:], scalar1=-1.0 / S_COLS, scalar2=None, op0=ALU.mult
+            )
+            return {"y": y, "minus_mean": minus_mean}
+
+        def vector_product(m):
             wide = psum.tile([P, BANK], F32, tag="acc")
             mx_group(nc, wide[:], w1, v_moving, m, slice(0, BANK))
             rest = psum.tile([P, V_COLS - BANK], F32, tag="acc")
@@ -307,112 +322,111 @@ def tile_feedforward_pb_kernel(
                 out=y[:, BANK:], in0=rest[:], scalar=1.0 / math.sqrt(V_HID), in1=v_parked[:, m, BANK:],
                 op0=ALU.mult, op1=ALU.add,
             )
-            squares = work.tile([P, V_COLS], F32, tag="squares")
-            sum_of_squares = small.tile([P, 1], F32)
-            nc.scalar.activation(out=squares[:], in_=y[:], func=ACT.Square, accum_out=sum_of_squares[:])
-            deviation = small.tile([P, 1], F32)
-            nc.scalar.activation(
-                out=deviation[:], in_=sum_of_squares[:], func=ACT.Sqrt, bias=eps[:], scale=1.0 / V_COLS
-            )
-            return {"y": y, "deviation": deviation}
+            return {"y": y}
 
-        def start_scalar_tile(m):
-            acc = psum.tile([P, S_COLS], F32, tag="acc")
-            bypass_group(nc, acc[:], bw0, s_feat_cols, m, slice(0, S_COLS))
-            y = work.tile([P, S_COLS], F32, tag="y")
-            total = small.tile([P, 1], F32)
-            nc.vector.scalar_tensor_tensor(
-                out=y[:], in0=acc[:], scalar=1.0 / math.sqrt(S_BYP), in1=s_parked[:, m, :],
-                op0=ALU.mult, op1=ALU.add, accum_out=total[:],
-            )
-            minus_mean = small.tile([P, 1], F32)
-            nc.vector.tensor_scalar(
-                out=minus_mean[:], in0=total[:], scalar1=-1.0 / S_COLS, scalar2=None, op0=ALU.mult
-            )
-            squares = work.tile([P, S_COLS], F32, tag="squares")
+        def inverse_deviation(kind, tile):
+            cols = S_COLS if kind == "s" else V_COLS
+            squares = work.tile([P, cols], F32, tag="squares")
             sum_of_squares = small.tile([P, 1], F32)
             nc.scalar.activation(
-                out=squares[:], in_=y[:], func=ACT.Square, bias=minus_mean[:], accum_out=sum_of_squares[:]
+                out=squares[:], in_=tile["y"][:], func=ACT.Square,
+                bias=tile["minus_mean"][:] if kind == "s" else 0.0, accum_out=sum_of_squares[:],
             )
-            deviation = small.tile([P, 1], F32)
-            nc.scalar.activation(
-                out=deviation[:], in_=sum_of_squares[:], func=ACT.Sqrt, bias=eps[:], scale=1.0 / S_COLS
-            )
-            return {"y": y, "deviation": deviation, "minus_mean": minus_mean}
-
-        def gain_over_deviation(started, t):
             inverse = small.tile([P, 1], F32)
-            nc.vector.reciprocal(out=inverse[:], in_=started["deviation"][:])
-            factor = small.tile([P, 1], F32)
-            nc.vector.tensor_tensor(out=factor[:], in0=inverse[:], in1=norm_cols[:, t : t + 1], op=ALU.mult)
-            return factor
-
-        def norm_vector_tile(m, started):
-            factor = gain_over_deviation(started, S_TILES + m)
-            z = work.tile([P, V_COLS], F32, tag="z")
-            nc.gpsimd.tensor_scalar(
-                out=z[:], in0=started["y"][:], scalar1=factor[:], scalar2=0.0, op0=ALU.mult, op1=ALU.add
+            nc.scalar.activation(
+                out=inverse[:], in_=sum_of_squares[:], func=ACT.Abs_reciprocal_sqrt, bias=eps[:], scale=1.0 / cols
             )
-            return z
+            tile["inverse"] = inverse
 
-        def norm_scalar_tile(m, started):
-            factor = gain_over_deviation(started, m)
-            shift = small.tile([P, 1], F32)
-            nc.vector.scalar_tensor_tensor(
-                out=shift[:], in0=started["minus_mean"][:], scalar=factor[:],
-                in1=norm_cols[:, GAINS + m : GAINS + m + 1], op0=ALU.mult, op1=ALU.add,
-            )
-            z = work.tile([P, S_COLS], F32, tag="z")
-            nc.gpsimd.tensor_scalar(
-                out=z[:], in0=started["y"][:], scalar1=factor[:], scalar2=shift[:], op0=ALU.mult, op1=ALU.add
-            )
-            return z
+        def norm(kind, m, tile):
+            if kind == "s":
+                unit = work.tile([P, S_COLS], F32, tag="unit")
+                nc.vector.tensor_scalar(
+                    out=unit[:], in0=tile["y"][:], scalar1=tile["minus_mean"][:], scalar2=tile["inverse"][:],
+                    op0=ALU.add, op1=ALU.mult,
+                )
+                z = work.tile([P, S_COLS], F32, tag="z")
+                nc.vector.tensor_scalar(
+                    out=z[:], in0=unit[:], scalar1=norm_cols[:, m : m + 1],
+                    scalar2=norm_cols[:, GAINS + m : GAINS + m + 1], op0=ALU.mult, op1=ALU.add,
+                )
+            else:
+                z = work.tile([P, V_COLS], F32, tag="z")
+                nc.vector.tensor_scalar(
+                    out=z[:], in0=tile["y"][:], scalar1=tile["inverse"][:],
+                    scalar2=norm_cols[:, S_TILES + m : S_TILES + m + 1], op0=ALU.mult, op1=ALU.mult,
+                )
+            tile["z"] = z
 
-        def store_vector_tile(m, z):
+        def transpose_vector_tile(m, z):
+            banks = []
             for h in range(HALVES):
-                bank = psum.tile([P, 4, P], F32, tag="tr")
+                bank = psum.tile([P, 4, P], F32, tag="tr", name="v_rows_bank")
                 for d in range(DV):
                     nc.tensor.transpose(bank[:, d, :], z[:, block(DV * h + d)], identity[:])
-                rows = work.tile([P, P, DV], F32, tag="rows")
-                copy_words(nc, h, out=rows[:], in_=bank[:, 0:DV, :].rearrange("n d o -> n o d"))
-                first = S_OUT + DV * P * m
-                nc.sync.dma_start(
-                    out=out[half_rows(h), first : first + DV * P], in_=rows[:].rearrange("n o d -> n (o d)")
-                )
+                banks.append(bank)
+            return banks
 
-        s_bank = {}
+        def store_vector_half(m, h, bank, copy):
+            rows = work.tile([P, P, DV], F32, tag="rows")
+            copy(out=rows[:], in_=bank[:, 0:DV, :].rearrange("n d o -> n o d"))
+            first = S_OUT + DV * P * m
+            nc.sync.dma_start(
+                out=out[half_rows(h), first : first + DV * P], in_=rows[:].rearrange("n o d -> n (o d)")
+            )
 
-        def store_scalar_tile(m, z):
-            place = m % 2
-            if place == 0:
-                s_bank[0] = psum.tile([P, HALVES, 2, P], F32, tag="tr", name="pair_bank")
-            for h in range(HALVES):
-                nc.tensor.transpose(s_bank[0][:, h, place, :], z[:, block(h)], identity[:])
-            if place == 1:
-                rows = work.tile([P, HALVES, 2, P], F32, tag="rows")
-                nc.scalar.copy(out=rows[:], in_=s_bank[0][:])
-                nc.sync.dma_start(
-                    out=out.rearrange("(h n) c -> n h c", n=P)[:, :, P * (m - 1) : P * (m + 1)],
-                    in_=rows[:].rearrange("n h m o -> n h (m o)"),
-                )
+        def transpose_scalar_tiles(zs):
+            bank = psum.tile([P, HALVES, len(zs), P], F32, tag="tr")
+            for i in range(len(zs)):
+                for h in range(HALVES):
+                    nc.tensor.transpose(bank[:, h, i, :], zs[i][:, block(h)], identity[:])
+            return bank
 
-        order = []
-        for m in range(V_TILES):
+        def store_scalar_tiles(m, count, bank):
+            rows = work.tile([P, HALVES, count, P], F32, tag="rows")
+            nc.scalar.copy(out=rows[:], in_=bank[:])
+            nc.sync.dma_start(
+                out=out.rearrange("(h n) c -> n h c", n=P)[:, :, P * m : P * (m + count)],
+                in_=rows[:].rearrange("n h m o -> n h (m o)"),
+            )
+
+        order = [("s", 0), ("v", 0), ("s", 1)]
+        for m in range(1, V_TILES):
             order.extend([("v", m), ("s", 2 * m), ("s", 2 * m + 1)])
-        started = {}
-        normed = {}
-        for i in range(len(order) + LAG):
-            if i < len(order):
-                kind, m = order[i]
-                started[i] = start_vector_tile(m) if kind == "v" else start_scalar_tile(m)
-            j = i - 1
-            if 0 <= j < len(order):
-                kind, m = order[j]
-                normed[j] = norm_vector_tile(m, started[j]) if kind == "v" else norm_scalar_tile(m, started[j])
-            j = i - LAG
-            if j >= 0:
-                kind, m = order[j]
-                if kind == "v":
-                    store_vector_tile(m, normed[j])
-                else:
-                    store_scalar_tile(m, normed[j])
+        tiles = {}
+
+        banks = {}
+
+        def transpose_group(j):
+            banks["v"] = transpose_vector_tile(j, tiles["v", j]["z"])
+            banks["s"] = transpose_scalar_tiles([tiles["s", 2 * j]["z"], tiles["s", 2 * j + 1]["z"]])
+
+        def store_group(j):
+            for h in range(HALVES):
+                store_vector_half(j, h, banks["v"][h], nc.scalar.copy)
+            store_scalar_tiles(2 * j, 2, banks["s"])
+
+        for i in range(len(order)):
+            kind, m = order[i]
+            place = i % 3
+            norm_first = place == 2 and order[i - 1][0] == "s"
+            if norm_first:
+                norm(*order[i - 1], tiles[order[i - 1]])
+            tiles[kind, m] = scalar_product(m) if kind == "s" else vector_product(m)
+            stores = place == 1 and i > 3
+            if stores:
+                transpose_group(i // 3 - 1)
+            inverse_deviation(kind, tiles[kind, m])
+            if stores:
+                store_group(i // 3 - 1)
+            if i > 0 and not norm_first:
+                norm(*order[i - 1], tiles[order[i - 1]])
+        last = V_TILES - 1
+        v_banks = transpose_vector_tile(last, tiles["v", last]["z"])
+        s_bank = transpose_scalar_tiles([tiles["s", 2 * last]["z"]])
+        store_vector_half(last, 0, v_banks[0], nc.vector.tensor_copy)
+        store_vector_half(last, 1, v_banks[1], nc.scalar.copy)
+        store_scalar_tiles(2 * last, 1, s_bank)
+        norm(*order[-1], tiles[order[-1]])
+        s_bank = transpose_scalar_tiles([tiles["s", 2 * last + 1]["z"]])
+        store_scalar_tiles(2 * last + 1, 1, s_bank)

@@ -141,17 +141,21 @@ def tile_feedforward_pb_kernel(
         warm = keep.tile([P, 1], F32)
         nc.scalar.activation(out=warm[:], in_=eps[:], func=ACT.Abs_reciprocal_sqrt)
 
-        for h in range(HALVES):
-            nc.sync.dma_start(out=h2s[h][:], in_=h2[half_rows(h), 0:S_HID])
-        load_scale_rows(nc, w0["planes"], lin3_W0_scales)
         w0_in = lin3_W0_words.rearrange("g p b -> p g b")
-        for part in range(2):
-            some = slice(S_OUT * part, S_OUT * (part + 1))
-            nc.sync.dma_start(out=w0["words"][:, :, some].bitcast(I32), in_=w0_in[:, :, some].bitcast(I32))
-        nc.scalar.dma_start(out=norm_rows[0:GAINS, :], in_=bn_weight.rearrange("(r c) -> r c", c=P))
-        nc.scalar.dma_start(
-            out=norm_rows[GAINS : GAINS + S_TILES, :], in_=bn_bias.rearrange("(r c) -> r c", c=P)
-        )
+        w0_half = [slice(S_OUT * part, S_OUT * (part + 1)) for part in range(2)]
+
+        def load_w0_words(part):
+            nc.sync.dma_start(
+                out=w0["words"][:, :, w0_half[part]].bitcast(I32), in_=w0_in[:, :, w0_half[part]].bitcast(I32)
+            )
+
+        for piece in range(2):
+            cols = slice(S_HID // 2 * piece, S_HID // 2 * (piece + 1))
+            nc.sync.dma_start(out=h2s[0][:, cols], in_=h2[half_rows(0), cols])
+        load_scale_rows(nc, w0["planes"], lin3_W0_scales)
+        load_w0_words(0)
+        nc.sync.dma_start(out=h2s[1][:], in_=h2[half_rows(1), 0:S_HID])
+        load_w0_words(1)
         for h in range(HALVES):
             nc.sync.dma_start(out=fv[h][:], in_=features[half_rows(h), S_BYP:])
         nc.sync.dma_start(out=bw1[:], in_=byp_W1.rearrange("(c q e) o -> q c e o", q=P, e=2))
@@ -164,14 +168,22 @@ def tile_feedforward_pb_kernel(
             out=w1["words"][:].bitcast(I32),
             in_=lin3_W1_words.rearrange("g p b -> p g b").bitcast(I32),
         )
+        nc.sync.dma_start(out=norm_rows[0:GAINS, :], in_=bn_weight.rearrange("(r c) -> r c", c=P))
+        nc.sync.dma_start(
+            out=norm_rows[GAINS : GAINS + S_TILES, :], in_=bn_bias.rearrange("(r c) -> r c", c=P)
+        )
         nc.sync.dma_start(out=bw0[:], in_=byp_W0.rearrange("(c q e) o -> q c e o", q=P, e=2))
 
-        s_grouped = keep.tile([P, S_PASSES, S_COLS, 4], BF16, align_bytes=64)
-        s_moving = {
-            "codes": keep.tile([P, S_PASSES, S_COLS], U32, name="s_codes", align_bytes=64),
-            "planes": keep.tile([P, S_PASSES, S_COLS], U8, name="s_planes", align_bytes=64),
-        }
-        for h in range(HALVES):
+        s_grouped = [keep.tile([P, S_PASSES, P, 4], BF16, name="s_grouped%d" % h, align_bytes=64) for h in range(HALVES)]
+        s_moving = [
+            {
+                "codes": keep.tile([P, S_PASSES, P], U32, name="s_codes%d" % h, align_bytes=64),
+                "planes": keep.tile([P, S_PASSES, P], U8, name="s_planes%d" % h, align_bytes=64),
+            }
+            for h in range(HALVES)
+        ]
+
+        def transpose_h2_scalars(h):
             words = h2s[h][:].bitcast(F32).rearrange("n (g q u) -> n g u q", q=P, u=2)
             for g0 in range(0, S_PASSES, 2):
                 bank = transpose_four(
@@ -180,35 +192,53 @@ def tile_feedforward_pb_kernel(
                 copy_words(
                     nc,
                     g0 // 2,
-                    out=s_grouped[:].bitcast(F32)[:, g0 : g0 + 2, block(h), :],
+                    out=s_grouped[h][:].bitcast(F32)[:, g0 : g0 + 2, :, :],
                     in_=bank[:].rearrange("q (g u) n -> q g n u", u=2),
                 )
-            for g in range(S_PASSES):
-                nc.vector.quantize_mx(
-                    out=s_moving["codes"][:, g, block(h)].bitcast(FP8X4),
-                    scales=s_moving["planes"][:, g, block(h)],
-                    in_=s_grouped[:, g, block(h), :].rearrange("q n t -> q (n t)"),
-                )
 
-        norm_rows_f32 = keep.tile([P, P], F32)
-        nc.vector.tensor_copy(out=norm_rows_f32[:], in_=norm_rows[:])
+        def quantise_h2_scalars(h):
+            for g0 in range(0, S_PASSES, 2):
+                nc.vector.quantize_mx(
+                    out=s_moving[h]["codes"][:, g0 : g0 + 2, :].rearrange("q g n -> q (g n)").bitcast(FP8X4),
+                    scales=s_moving[h]["planes"][:, g0 : g0 + 2, :].rearrange("q g n -> q (g n)"),
+                    in_=s_grouped[h][:, g0 : g0 + 2, :, :].rearrange("q g n t -> q (g n t)"),
+                )
 
         s_parked = keep.tile([P, S_TILES, S_COLS], F32)
         s_acc = [psum.tile([P, 2, S_COLS], F32, tag="acc", name="s_acc") for pair in range(S_TILES // 2)]
-        for h in range(HALVES):
-            for m in range(S_TILES):
-                mx_group(nc, s_acc[m // 2][:, m % 2, block(h)], w0, s_moving, m, block(h))
-        for pair in range(S_TILES // 2):
-            nc.scalar.activation(
-                out=s_parked[:, 2 * pair : 2 * pair + 2, :], in_=s_acc[pair][:], func=ACT.Copy,
-                scale=1.0 / math.sqrt(S_HID),
+
+        def scalar_mx_groups(tiles, h):
+            for m in tiles:
+                mx_group(nc, s_acc[m // 2][:, m % 2, block(h)], w0, s_moving[h], m, slice(0, P))
+
+        def park_scalars(pair):
+            dst = s_parked[:, 2 * pair : 2 * pair + 2, :]
+            if pair % 2 == 0:
+                nc.vector.tensor_scalar(
+                    out=dst, in0=s_acc[pair][:], scalar1=1.0 / math.sqrt(S_HID), scalar2=None, op0=ALU.mult
+                )
+            else:
+                nc.scalar.activation(
+                    out=dst, in_=s_acc[pair][:], func=ACT.Copy, scale=1.0 / math.sqrt(S_HID)
+                )
+
+        s_feat = keep.tile([P, S_CHUNKS, 2 * S_COLS], BF16)
+
+        def transpose_feature_scalars(h):
+            bank = transpose_four(
+                nc, psum, identity, [fs[h][:].bitcast(F32)[:, block(c)] for c in range(S_CHUNKS)]
             )
+            copy_words(nc, h, out=s_feat[:].bitcast(F32)[:, :, block(h)], in_=bank[:])
 
         f_sorted = [keep.tile([P, DV, V_BYP], BF16, name="f_sorted%d" % h) for h in range(HALVES)]
-        for h in range(HALVES):
-            nc.vector.tensor_copy(out=f_sorted[h][:], in_=fv[h][:].rearrange("n (i d) -> n d i", d=DV))
         v_feat = keep.tile([P, V_CHUNKS, 2 * V_COLS], BF16)
-        for d in range(DV):
+
+        def sort_feature_vectors(h):
+            by_part = fv[h][:].rearrange("n (i d) -> n d i", d=DV)
+            nc.vector.tensor_copy(out=f_sorted[h][:, 0:2, :], in_=by_part[:, 0:2, :])
+            nc.scalar.copy(out=f_sorted[h][:, 2, :], in_=by_part[:, 2, :])
+
+        def transpose_feature_vectors(d):
             bank = transpose_four(
                 nc,
                 psum,
@@ -221,19 +251,27 @@ def tile_feedforward_pb_kernel(
                 out=v_feat[:].bitcast(F32).rearrange("q c (h d n) -> q c h d n", h=HALVES, d=DV)[:, :, :, d, :],
                 in_=bank[:].rearrange("q (h c) n -> q c h n", c=V_CHUNKS),
             )
-        s_feat = keep.tile([P, S_CHUNKS, 2 * S_COLS], BF16)
+
+        transpose_h2_scalars(0)
+        quantise_h2_scalars(0)
+        scalar_mx_groups(range(0, S_TILES // 2), 0)
+        transpose_h2_scalars(1)
+        quantise_h2_scalars(1)
+        scalar_mx_groups(range(S_TILES // 2, S_TILES), 0)
         for h in range(HALVES):
-            bank = transpose_four(
-                nc, psum, identity, [fs[h][:].bitcast(F32)[:, block(c)] for c in range(S_CHUNKS)]
-            )
-            copy_words(nc, h + 1, out=s_feat[:].bitcast(F32)[:, :, block(h)], in_=bank[:])
+            sort_feature_vectors(h)
+        scalar_mx_groups(range(0, S_TILES - 2), 1)
+        park_scalars(0)
+        park_scalars(1)
+        for d in range(DV):
+            transpose_feature_vectors(d)
+        scalar_mx_groups(range(S_TILES - 2, S_TILES), 1)
+        for h in range(HALVES):
+            transpose_feature_scalars(h)
+        park_scalars(2)
+        park_scalars(3)
         v_feat_cols = v_feat[:].rearrange("q c (n e) -> q c n e", e=2)
         s_feat_cols = s_feat[:].rearrange("q c (n e) -> q c n e", e=2)
-
-        norm_bank = psum.tile([P, 4, P], F32, tag="tr")
-        nc.tensor.transpose(norm_bank[:, 0, :], norm_rows_f32[:], identity[:])
-        norm_cols = keep.tile([P, GAINS + S_TILES], F32)
-        nc.vector.tensor_copy(out=norm_cols[:], in_=norm_bank[:, 0, 0 : GAINS + S_TILES])
 
         v_sorted = [keep.tile([P, DV, 2 * V_PASSES, 2 * P], BF16, name="v_sorted%d" % h) for h in range(HALVES)]
         for h in range(HALVES):
@@ -247,6 +285,10 @@ def tile_feedforward_pb_kernel(
                         nc.vector.tensor_copy(out=dst, in_=by_part[:, d, g])
                     else:
                         nc.scalar.copy(out=dst, in_=by_part[:, d, g])
+
+        norm_rows_f32 = keep.tile([P, P], F32)
+        nc.vector.tensor_copy(out=norm_rows_f32[:], in_=norm_rows[:])
+        norm_cols = keep.tile([P, GAINS + S_TILES], F32)
 
         v_grouped = keep.tile([P, V_PASSES, V_COLS, 4], BF16, align_bytes=64)
         v_moving = {
@@ -266,9 +308,9 @@ def tile_feedforward_pb_kernel(
                 )
 
         def quantise_h2_vectors(h):
-            for d in range(DV):
+            for first, count in (0, 2), (2, 1):
                 for g in range(V_PASSES):
-                    cols = block(DV * h + d)
+                    cols = slice(P * (DV * h + first), P * (DV * h + first + count))
                     nc.vector.quantize_mx(
                         out=v_moving["codes"][:, g, cols].bitcast(FP8X4),
                         scales=v_moving["planes"][:, g, cols],
@@ -289,6 +331,10 @@ def tile_feedforward_pb_kernel(
             )
             if 1 <= m <= HALVES:
                 transpose_h2_vectors(m - 1)
+            if m == HALVES:
+                norm_bank = psum.tile([P, 4, P], F32, tag="tr")
+                nc.tensor.transpose(norm_bank[:, 0, :], norm_rows_f32[:], identity[:])
+                nc.vector.tensor_copy(out=norm_cols[:], in_=norm_bank[:, 0, 0 : GAINS + S_TILES])
             if 2 <= m <= HALVES + 1:
                 quantise_h2_vectors(m - 2)
 

@@ -66,10 +66,12 @@ def copy_words(nc, turn, out, in_):
 
 def mx_group(nc, acc, weight, moving, m, cols):
     passes = weight["passes"]
+    share = weight["words"][0].shape[2] // 2
+    words, first = weight["words"][P * m // share], 2 * (P * m % share)
     for g in range(passes):
         nc.tensor.matmul_mx(
             out=acc,
-            lhsT=weight["words"][:, g, 2 * P * m : 2 * P * (m + 1)].bitcast(FP4X4),
+            lhsT=words[:, g, first : first + 2 * P].bitcast(FP4X4),
             lhsT_scale=weight["planes"][:, g, block(m)],
             rhs=moving["codes"][:, g, cols].bitcast(FP8X4),
             rhs_scale=moving["planes"][:, g, cols],
@@ -78,14 +80,14 @@ def mx_group(nc, acc, weight, moving, m, cols):
         )
 
 
-def bypass_group(nc, acc, weights, moving, m, cols):
+def bypass_group(nc, acc, weights, moving, m):
     chunks = weights.shape[1]
     for c in range(chunks):
         for e in range(2):
             nc.tensor.matmul(
                 out=acc,
                 lhsT=weights[:, c, e, block(m)],
-                rhs=moving[:, c, cols, e],
+                rhs=moving[:, c, :, e],
                 start=(c == 0 and e == 0),
                 stop=(c == chunks - 1 and e == 1),
             )
@@ -118,12 +120,12 @@ def tile_feedforward_pb_kernel(
         fs = [keep.tile([P, S_BYP], BF16, name="fs%d" % h) for h in range(HALVES)]
         fv = [keep.tile([P, DV * V_BYP], BF16, name="fv%d" % h) for h in range(HALVES)]
         w0 = {
-            "words": keep.tile([P, S_PASSES, 2 * S_OUT], U8, name="w0_words", align_bytes=64),
+            "words": [keep.tile([P, S_PASSES, S_OUT], U8, name="w0_words%d" % part, align_bytes=64) for part in range(2)],
             "planes": keep.tile([P, S_PASSES, S_OUT], U8, name="w0_planes", align_bytes=64),
             "passes": S_PASSES,
         }
         w1 = {
-            "words": keep.tile([P, V_PASSES, 2 * V_OUT], U8, name="w1_words", align_bytes=64),
+            "words": [keep.tile([P, V_PASSES, 2 * V_OUT], U8, name="w1_words", align_bytes=64)],
             "planes": keep.tile([P, V_PASSES, V_OUT], U8, name="w1_planes", align_bytes=64),
             "passes": V_PASSES,
         }
@@ -136,18 +138,24 @@ def tile_feedforward_pb_kernel(
         nc.vector.memset(eps[:], EPS)
         norm_rows = keep.tile([P, P], BF16)
         nc.vector.memset(norm_rows[:], 0.0)
-        identity = keep.tile([P, P], F32)
-        make_identity(nc, identity[:])
         warm = keep.tile([P, 1], F32)
         nc.scalar.activation(out=warm[:], in_=eps[:], func=ACT.Abs_reciprocal_sqrt)
 
+        zeros = keep.tile([P, BANK], BF16)
+        nc.gpsimd.memset(zeros[:], 0.0)
+        identity = keep.tile([P, P], F32)
+        make_identity(nc, identity[:])
+
+        def idle_products(count):
+            bank = psum.tile([P, BANK], F32, tag="tr", name="idle_bank")
+            for i in range(count):
+                nc.tensor.matmul(out=bank[:], lhsT=zeros[:, 0:P], rhs=zeros[:], start=True, stop=True)
+
         w0_in = lin3_W0_words.rearrange("g p b -> p g b")
-        w0_half = [slice(S_OUT * part, S_OUT * (part + 1)) for part in range(2)]
 
         def load_w0_words(part):
-            nc.sync.dma_start(
-                out=w0["words"][:, :, w0_half[part]].bitcast(I32), in_=w0_in[:, :, w0_half[part]].bitcast(I32)
-            )
+            half = slice(S_OUT * part, S_OUT * (part + 1))
+            nc.sync.dma_start(out=w0["words"][part][:].bitcast(I32), in_=w0_in[:, :, half].bitcast(I32))
 
         for piece in range(2):
             cols = slice(S_HID // 2 * piece, S_HID // 2 * (piece + 1))
@@ -165,7 +173,7 @@ def tile_feedforward_pb_kernel(
             nc.sync.dma_start(out=h2v[h][:], in_=h2[half_rows(h), S_HID:])
         load_scale_rows(nc, w1["planes"], lin3_W1_scales)
         nc.sync.dma_start(
-            out=w1["words"][:].bitcast(I32),
+            out=w1["words"][0][:].bitcast(I32),
             in_=lin3_W1_words.rearrange("g p b -> p g b").bitcast(I32),
         )
         nc.sync.dma_start(out=norm_rows[0:GAINS, :], in_=bn_weight.rearrange("(r c) -> r c", c=P))
@@ -222,38 +230,50 @@ def tile_feedforward_pb_kernel(
                     out=dst, in_=s_acc[pair][:], func=ACT.Copy, scale=1.0 / math.sqrt(S_HID)
                 )
 
-        s_feat = keep.tile([P, S_CHUNKS, 2 * S_COLS], BF16)
+        s_feat = keep.tile([P, S_CHUNKS, S_COLS, 2], BF16)
 
-        def transpose_feature_scalars(h):
+        def transpose_feature_scalars(pair):
+            chunks = slice(2 * pair, 2 * pair + 2)
             bank = transpose_four(
-                nc, psum, identity, [fs[h][:].bitcast(F32)[:, block(c)] for c in range(S_CHUNKS)]
+                nc,
+                psum,
+                identity,
+                [fs[h][:].bitcast(F32)[:, block(c)] for c in range(2 * pair, 2 * pair + 2) for h in range(HALVES)],
             )
-            copy_words(nc, h, out=s_feat[:].bitcast(F32)[:, :, block(h)], in_=bank[:])
+            copy_words(
+                nc,
+                pair,
+                out=s_feat[:, chunks, :, :].rearrange("q c n e -> q (c n e)").bitcast(F32),
+                in_=bank[:].rearrange("q b n -> q (b n)"),
+            )
 
         f_sorted = [keep.tile([P, DV, V_BYP], BF16, name="f_sorted%d" % h) for h in range(HALVES)]
-        v_feat = keep.tile([P, V_CHUNKS, 2 * V_COLS], BF16)
+        v_feat_wide = keep.tile([P, V_CHUNKS, BANK, 2], BF16)
+        v_feat_rest = keep.tile([P, V_CHUNKS, V_COLS - BANK, 2], BF16)
 
         def sort_feature_vectors(h):
             by_part = fv[h][:].rearrange("n (i d) -> n d i", d=DV)
             nc.vector.tensor_copy(out=f_sorted[h][:, 0:2, :], in_=by_part[:, 0:2, :])
             nc.scalar.copy(out=f_sorted[h][:, 2, :], in_=by_part[:, 2, :])
 
-        def transpose_feature_vectors(d):
+        def transpose_feature_vectors(turn, chunks, blocks, out):
             bank = transpose_four(
                 nc,
                 psum,
                 identity,
-                [f_sorted[h][:].bitcast(F32)[:, d, block(c)] for h in range(HALVES) for c in range(V_CHUNKS)],
+                [f_sorted[b // DV][:].bitcast(F32)[:, b % DV, block(c)] for c in chunks for b in blocks],
             )
             copy_words(
                 nc,
-                d,
-                out=v_feat[:].bitcast(F32).rearrange("q c (h d n) -> q c h d n", h=HALVES, d=DV)[:, :, :, d, :],
-                in_=bank[:].rearrange("q (h c) n -> q c h n", c=V_CHUNKS),
+                turn,
+                out=out.rearrange("q c n e -> q (c n e)").bitcast(F32),
+                in_=bank[:].rearrange("q b n -> q (b n)"),
             )
 
+        idle_products(3)
         transpose_h2_scalars(0)
         quantise_h2_scalars(0)
+        idle_products(3)
         scalar_mx_groups(range(0, S_TILES // 2), 0)
         transpose_h2_scalars(1)
         quantise_h2_scalars(1)
@@ -263,18 +283,17 @@ def tile_feedforward_pb_kernel(
         scalar_mx_groups(range(0, S_TILES - 2), 1)
         park_scalars(0)
         park_scalars(1)
-        for d in range(DV):
-            transpose_feature_vectors(d)
+        for c in range(V_CHUNKS):
+            transpose_feature_vectors(c, [c], range(BANK // P), v_feat_wide[:, c : c + 1, :, :])
+        transpose_feature_vectors(V_CHUNKS, range(V_CHUNKS), range(BANK // P, V_COLS // P), v_feat_rest[:])
         scalar_mx_groups(range(S_TILES - 2, S_TILES), 1)
-        for h in range(HALVES):
-            transpose_feature_scalars(h)
+        for pair in range(S_CHUNKS // 2):
+            transpose_feature_scalars(pair)
         park_scalars(2)
         park_scalars(3)
-        v_feat_cols = v_feat[:].rearrange("q c (n e) -> q c n e", e=2)
-        s_feat_cols = s_feat[:].rearrange("q c (n e) -> q c n e", e=2)
 
         v_sorted = [keep.tile([P, DV, 2 * V_PASSES, 2 * P], BF16, name="v_sorted%d" % h) for h in range(HALVES)]
-        for h in range(HALVES):
+        def sort_h2_vectors(h):
             by_part = h2v[h][:].rearrange(
                 "n (g q u e d) -> n d g u q e", g=V_PASSES, q=P, u=2, e=2, d=DV
             )
@@ -287,10 +306,15 @@ def tile_feedforward_pb_kernel(
                         nc.scalar.copy(out=dst, in_=by_part[:, d, g])
 
         norm_rows_f32 = keep.tile([P, P], F32)
-        nc.vector.tensor_copy(out=norm_rows_f32[:], in_=norm_rows[:])
         norm_cols = keep.tile([P, GAINS + S_TILES], F32)
 
-        v_grouped = keep.tile([P, V_PASSES, V_COLS, 4], BF16, align_bytes=64)
+        v_grouped = [
+            [keep.tile([P, 2, P, 4], BF16, name="v_grouped%d_%d" % (h, g), align_bytes=64) for g in range(V_PASSES)]
+            for h in range(HALVES)
+        ]
+        v_grouped_last = [
+            keep.tile([P, V_PASSES, P, 4], BF16, name="v_grouped_last%d" % h, align_bytes=64) for h in range(HALVES)
+        ]
         v_moving = {
             "codes": keep.tile([P, V_PASSES, V_COLS], U32, name="v_codes", align_bytes=64),
             "planes": keep.tile([P, V_PASSES, V_COLS], U8, name="v_planes", align_bytes=64),
@@ -298,49 +322,54 @@ def tile_feedforward_pb_kernel(
 
         def transpose_h2_vectors(h):
             words = v_sorted[h][:].bitcast(F32)
-            for d in range(DV):
-                bank = transpose_four(nc, psum, identity, [words[:, d, j, :] for j in range(4)])
+            for turn in range(DV):
+                if turn < V_PASSES:
+                    blocks, dst = [words[:, d, 2 * turn + u, :] for d in range(2) for u in range(2)], v_grouped[h][turn]
+                else:
+                    blocks, dst = [words[:, 2, j, :] for j in range(4)], v_grouped_last[h]
+                bank = transpose_four(nc, psum, identity, blocks)
                 copy_words(
-                    nc,
-                    d,
-                    out=v_grouped[:].bitcast(F32)[:, :, block(DV * h + d), :],
-                    in_=bank[:].rearrange("q (g u) n -> q g n u", u=2),
+                    nc, turn, out=dst[:].bitcast(F32), in_=bank[:].rearrange("q (a u) n -> q a n u", u=2)
                 )
 
         def quantise_h2_vectors(h):
-            for first, count in (0, 2), (2, 1):
-                for g in range(V_PASSES):
-                    cols = slice(P * (DV * h + first), P * (DV * h + first + count))
+            for g in range(V_PASSES):
+                for first, src in (0, v_grouped[h][g][:]), (2, v_grouped_last[h][:, g : g + 1, :, :]):
+                    cols = slice(P * (DV * h + first), P * (DV * h + first + src.shape[1]))
                     nc.vector.quantize_mx(
                         out=v_moving["codes"][:, g, cols].bitcast(FP8X4),
                         scales=v_moving["planes"][:, g, cols],
-                        in_=v_grouped[:, g, cols, :].rearrange("q n t -> q (n t)"),
+                        in_=src.rearrange("q a n t -> q (a n t)"),
                     )
 
         v_parked = keep.tile([P, V_TILES, V_COLS], F32)
+        sort_h2_vectors(0)
         for m in range(V_TILES):
+            if m >= HALVES:
+                quantise_h2_vectors(m - HALVES)
             wide = psum.tile([P, BANK], F32, tag="acc")
-            bypass_group(nc, wide[:], bw1, v_feat_cols, m, slice(0, BANK))
+            bypass_group(nc, wide[:], bw1, v_feat_wide, m)
             rest = psum.tile([P, V_COLS - BANK], F32, tag="acc")
-            bypass_group(nc, rest[:], bw1, v_feat_cols, m, slice(BANK, V_COLS))
+            bypass_group(nc, rest[:], bw1, v_feat_rest, m)
             nc.scalar.activation(
                 out=v_parked[:, m, 0:BANK], in_=wide[:], func=ACT.Copy, scale=1.0 / math.sqrt(V_BYP)
             )
-            nc.scalar.activation(
-                out=v_parked[:, m, BANK:], in_=rest[:], func=ACT.Copy, scale=1.0 / math.sqrt(V_BYP)
+            nc.vector.tensor_scalar(
+                out=v_parked[:, m, BANK:], in0=rest[:], scalar1=1.0 / math.sqrt(V_BYP), scalar2=None, op0=ALU.mult
             )
+            if m == 0:
+                sort_h2_vectors(1)
+                nc.vector.tensor_copy(out=norm_rows_f32[:], in_=norm_rows[:])
             if 1 <= m <= HALVES:
                 transpose_h2_vectors(m - 1)
             if m == HALVES:
                 norm_bank = psum.tile([P, 4, P], F32, tag="tr")
                 nc.tensor.transpose(norm_bank[:, 0, :], norm_rows_f32[:], identity[:])
                 nc.vector.tensor_copy(out=norm_cols[:], in_=norm_bank[:, 0, 0 : GAINS + S_TILES])
-            if 2 <= m <= HALVES + 1:
-                quantise_h2_vectors(m - 2)
 
         def scalar_product(m):
             acc = psum.tile([P, S_COLS], F32, tag="acc")
-            bypass_group(nc, acc[:], bw0, s_feat_cols, m, slice(0, S_COLS))
+            bypass_group(nc, acc[:], bw0, s_feat, m)
             y = work.tile([P, S_COLS], F32, tag="y")
             total = small.tile([P, 1], F32)
             nc.vector.scalar_tensor_tensor(

@@ -31,6 +31,7 @@ BANK = 512
 GAINS = S_TILES + V_TILES
 EPS = 1e-5
 
+ROWS_BUFS = 12
 WORK_BUFS = 6
 
 FLOPS = 2 * NODES * (S_HID * S_OUT + DV * V_HID * V_OUT + S_BYP * S_OUT + DV * V_BYP * V_OUT)
@@ -66,13 +67,13 @@ def copy_words(nc, turn, out, in_):
 
 def mx_group(nc, acc, weight, moving, m, cols):
     passes = weight["passes"]
-    share = weight["words"][0].shape[2] // 2
-    words, first = weight["words"][P * m // share], 2 * (P * m % share)
+    share = weight["planes"][0].shape[2]
+    words, planes, first = weight["words"][P * m // share], weight["planes"][P * m // share], P * m % share
     for g in range(passes):
         nc.tensor.matmul_mx(
             out=acc,
-            lhsT=words[:, g, first : first + 2 * P].bitcast(FP4X4),
-            lhsT_scale=weight["planes"][:, g, block(m)],
+            lhsT=words[:, g, 2 * first : 2 * (first + P)].bitcast(FP4X4),
+            lhsT_scale=planes[:, g, first : first + P],
             rhs=moving["codes"][:, g, cols].bitcast(FP8X4),
             rhs_scale=moving["planes"][:, g, cols],
             start=(g == 0),
@@ -81,12 +82,14 @@ def mx_group(nc, acc, weight, moving, m, cols):
 
 
 def bypass_group(nc, acc, weights, moving, m):
-    chunks = weights.shape[1]
+    share = weights[0].shape[3]
+    some, first = weights[P * m // share], P * m % share
+    chunks = some.shape[1]
     for c in range(chunks):
         for e in range(2):
             nc.tensor.matmul(
                 out=acc,
-                lhsT=weights[:, c, e, block(m)],
+                lhsT=some[:, c, e, first : first + P],
                 rhs=moving[:, c, :, e],
                 start=(c == 0 and e == 0),
                 stop=(c == chunks - 1 and e == 1),
@@ -121,19 +124,19 @@ def tile_feedforward_pb_kernel(
         fv = [keep.tile([P, DV * V_BYP], BF16, name="fv%d" % h) for h in range(HALVES)]
         w0 = {
             "words": [keep.tile([P, S_PASSES, S_OUT], U8, name="w0_words%d" % part, align_bytes=64) for part in range(2)],
-            "planes": keep.tile([P, S_PASSES, S_OUT], U8, name="w0_planes", align_bytes=64),
+            "planes": [keep.tile([P, S_PASSES, S_OUT // 2], U8, name="w0_planes%d" % part, align_bytes=64) for part in range(2)],
             "passes": S_PASSES,
         }
         w1 = {
             "words": [keep.tile([P, V_PASSES, 2 * V_OUT], U8, name="w1_words", align_bytes=64)],
-            "planes": keep.tile([P, V_PASSES, V_OUT], U8, name="w1_planes", align_bytes=64),
+            "planes": [keep.tile([P, V_PASSES, V_OUT], U8, name="w1_planes", align_bytes=64)],
             "passes": V_PASSES,
         }
-        bw0 = keep.tile([P, S_CHUNKS, 2, S_OUT], BF16)
-        bw1 = keep.tile([P, V_CHUNKS, 2, V_OUT], BF16)
+        bw0 = [keep.tile([P, S_CHUNKS, 2, S_OUT // 2], BF16, name="bw0_%d" % part) for part in range(2)]
+        bw1 = [keep.tile([P, V_CHUNKS, 2, V_OUT], BF16, name="bw1")]
 
-        nc.vector.memset(w0["planes"][:].bitcast(I32), 0)
-        nc.vector.memset(w1["planes"][:].bitcast(I32), 0)
+        for plane in w0["planes"] + w1["planes"]:
+            nc.vector.memset(plane[:].bitcast(I32), 0)
         eps = keep.tile([P, 1], F32)
         nc.vector.memset(eps[:], EPS)
         norm_rows = keep.tile([P, P], BF16)
@@ -153,25 +156,26 @@ def tile_feedforward_pb_kernel(
 
         w0_in = lin3_W0_words.rearrange("g p b -> p g b")
 
-        def load_w0_words(part):
+        def load_w0_half(part):
+            half = slice(S_OUT // 2 * part, S_OUT // 2 * (part + 1))
+            load_scale_rows(nc, w0["planes"][part], lin3_W0_scales[:, :, half])
             half = slice(S_OUT * part, S_OUT * (part + 1))
             nc.sync.dma_start(out=w0["words"][part][:].bitcast(I32), in_=w0_in[:, :, half].bitcast(I32))
 
         for piece in range(2):
             cols = slice(S_HID // 2 * piece, S_HID // 2 * (piece + 1))
             nc.sync.dma_start(out=h2s[0][:, cols], in_=h2[half_rows(0), cols])
-        load_scale_rows(nc, w0["planes"], lin3_W0_scales)
-        load_w0_words(0)
+        load_w0_half(0)
         nc.sync.dma_start(out=h2s[1][:], in_=h2[half_rows(1), 0:S_HID])
-        load_w0_words(1)
+        load_w0_half(1)
         for h in range(HALVES):
             nc.sync.dma_start(out=fv[h][:], in_=features[half_rows(h), S_BYP:])
-        nc.sync.dma_start(out=bw1[:], in_=byp_W1.rearrange("(c q e) o -> q c e o", q=P, e=2))
+        nc.sync.dma_start(out=bw1[0][:], in_=byp_W1.rearrange("(c q e) o -> q c e o", q=P, e=2))
         for h in range(HALVES):
             nc.sync.dma_start(out=fs[h][:], in_=features[half_rows(h), 0:S_BYP])
         for h in range(HALVES):
             nc.sync.dma_start(out=h2v[h][:], in_=h2[half_rows(h), S_HID:])
-        load_scale_rows(nc, w1["planes"], lin3_W1_scales)
+        load_scale_rows(nc, w1["planes"][0], lin3_W1_scales)
         nc.sync.dma_start(
             out=w1["words"][0][:].bitcast(I32),
             in_=lin3_W1_words.rearrange("g p b -> p g b").bitcast(I32),
@@ -180,7 +184,11 @@ def tile_feedforward_pb_kernel(
         nc.sync.dma_start(
             out=norm_rows[GAINS : GAINS + S_TILES, :], in_=bn_bias.rearrange("(r c) -> r c", c=P)
         )
-        nc.sync.dma_start(out=bw0[:], in_=byp_W0.rearrange("(c q e) o -> q c e o", q=P, e=2))
+        bw0_in = byp_W0.rearrange("(c q e) o -> q c e o", q=P, e=2)
+        for part in range(2):
+            half = slice(S_OUT // 2 * part, S_OUT // 2 * (part + 1))
+            for c in range(S_CHUNKS):
+                nc.sync.dma_start(out=bw0[part][:, c, :, :], in_=bw0_in[:, c, :, half])
 
         s_grouped = [keep.tile([P, S_PASSES, P, 4], BF16, name="s_grouped%d" % h, align_bytes=64) for h in range(HALVES)]
         s_moving = [
@@ -329,7 +337,7 @@ def tile_feedforward_pb_kernel(
                     blocks, dst = [words[:, 2, j, :] for j in range(4)], v_grouped_last[h]
                 bank = transpose_four(nc, psum, identity, blocks)
                 copy_words(
-                    nc, turn, out=dst[:].bitcast(F32), in_=bank[:].rearrange("q (a u) n -> q a n u", u=2)
+                    nc, turn + h, out=dst[:].bitcast(F32), in_=bank[:].rearrange("q (a u) n -> q a n u", u=2)
                 )
 
         def quantise_h2_vectors(h):
@@ -376,11 +384,14 @@ def tile_feedforward_pb_kernel(
                 out=y[:], in0=acc[:], scalar=1.0 / math.sqrt(S_BYP), in1=s_parked[:, m, :],
                 op0=ALU.mult, op1=ALU.add, accum_out=total[:],
             )
+            return {"y": y, "total": total}
+
+        def negate_mean(tile):
             minus_mean = small.tile([P, 1], F32)
             nc.vector.tensor_scalar(
-                out=minus_mean[:], in0=total[:], scalar1=-1.0 / S_COLS, scalar2=None, op0=ALU.mult
+                out=minus_mean[:], in0=tile["total"][:], scalar1=-1.0 / S_COLS, scalar2=None, op0=ALU.mult
             )
-            return {"y": y, "minus_mean": minus_mean}
+            tile["minus_mean"] = minus_mean
 
         def vector_product(m):
             wide = psum.tile([P, BANK], F32, tag="acc")
@@ -413,16 +424,19 @@ def tile_feedforward_pb_kernel(
             )
             tile["inverse"] = inverse
 
+        def center(tile):
+            unit = work.tile([P, S_COLS], F32, tag="unit")
+            nc.vector.tensor_scalar(
+                out=unit[:], in0=tile["y"][:], scalar1=tile["minus_mean"][:], scalar2=tile["inverse"][:],
+                op0=ALU.add, op1=ALU.mult,
+            )
+            tile["unit"] = unit
+
         def norm(kind, m, tile):
             if kind == "s":
-                unit = work.tile([P, S_COLS], F32, tag="unit")
-                nc.vector.tensor_scalar(
-                    out=unit[:], in0=tile["y"][:], scalar1=tile["minus_mean"][:], scalar2=tile["inverse"][:],
-                    op0=ALU.add, op1=ALU.mult,
-                )
                 z = work.tile([P, S_COLS], F32, tag="z")
                 nc.vector.tensor_scalar(
-                    out=z[:], in0=unit[:], scalar1=norm_cols[:, m : m + 1],
+                    out=z[:], in0=tile["unit"][:], scalar1=norm_cols[:, m : m + 1],
                     scalar2=norm_cols[:, GAINS + m : GAINS + m + 1], op0=ALU.mult, op1=ALU.add,
                 )
             else:
@@ -443,7 +457,7 @@ def tile_feedforward_pb_kernel(
             return banks
 
         def store_vector_half(m, h, bank, copy):
-            rows = work.tile([P, P, DV], F32, tag="rows")
+            rows = work.tile([P, P, DV], F32, tag="rows", bufs=ROWS_BUFS)
             copy(out=rows[:], in_=bank[:, 0:DV, :].rearrange("n d o -> n o d"))
             first = S_OUT + DV * P * m
             nc.sync.dma_start(
@@ -451,14 +465,14 @@ def tile_feedforward_pb_kernel(
             )
 
         def transpose_scalar_tiles(zs):
-            bank = psum.tile([P, HALVES, len(zs), P], F32, tag="tr")
+            bank = psum.tile([P, HALVES, len(zs), P], F32, tag="tr", name="s_rows_bank")
             for i in range(len(zs)):
                 for h in range(HALVES):
                     nc.tensor.transpose(bank[:, h, i, :], zs[i][:, block(h)], identity[:])
             return bank
 
         def store_scalar_tiles(m, count, bank):
-            rows = work.tile([P, HALVES, count, P], F32, tag="rows")
+            rows = work.tile([P, HALVES, count, P], F32, tag="rows", bufs=ROWS_BUFS)
             nc.scalar.copy(out=rows[:], in_=bank[:])
             nc.sync.dma_start(
                 out=out.rearrange("(h n) c -> n h c", n=P)[:, :, P * m : P * (m + count)],
@@ -469,7 +483,6 @@ def tile_feedforward_pb_kernel(
         for m in range(1, V_TILES):
             order.extend([("v", m), ("s", 2 * m), ("s", 2 * m + 1)])
         tiles = {}
-
         banks = {}
 
         def transpose_group(j):
@@ -484,24 +497,32 @@ def tile_feedforward_pb_kernel(
         for i in range(len(order)):
             kind, m = order[i]
             place = i % 3
-            norm_first = place == 2 and order[i - 1][0] == "s"
-            if norm_first:
-                norm(*order[i - 1], tiles[order[i - 1]])
+            before = order[i - 1] if i > 0 else None
+            norm_early = place == 2 and before[0] == "s"
+            if norm_early:
+                center(tiles[before])
             tiles[kind, m] = scalar_product(m) if kind == "s" else vector_product(m)
+            if norm_early:
+                norm(*before, tiles[before])
+            elif i > 0 and before[0] == "s":
+                center(tiles[before])
+            if kind == "s":
+                negate_mean(tiles[kind, m])
             stores = place == 1 and i > 3
             if stores:
                 transpose_group(i // 3 - 1)
             inverse_deviation(kind, tiles[kind, m])
             if stores:
                 store_group(i // 3 - 1)
-            if i > 0 and not norm_first:
-                norm(*order[i - 1], tiles[order[i - 1]])
+            if i > 0 and not norm_early:
+                norm(*before, tiles[before])
         last = V_TILES - 1
         v_banks = transpose_vector_tile(last, tiles["v", last]["z"])
         s_bank = transpose_scalar_tiles([tiles["s", 2 * last]["z"]])
         store_vector_half(last, 0, v_banks[0], nc.vector.tensor_copy)
         store_vector_half(last, 1, v_banks[1], nc.scalar.copy)
         store_scalar_tiles(2 * last, 1, s_bank)
+        center(tiles[order[-1]])
         norm(*order[-1], tiles[order[-1]])
         s_bank = transpose_scalar_tiles([tiles["s", 2 * last + 1]["z"]])
         store_scalar_tiles(2 * last + 1, 1, s_bank)

@@ -162,33 +162,37 @@ def tile_feedforward_pb_kernel(
             half = slice(S_OUT * part, S_OUT * (part + 1))
             nc.sync.dma_start(out=w0["words"][part][:].bitcast(I32), in_=w0_in[:, :, half].bitcast(I32))
 
+        bw0_in = byp_W0.rearrange("(c q e) o -> q c e o", q=P, e=2)
+
+        def load_bw0_half(part):
+            half = slice(S_OUT // 2 * part, S_OUT // 2 * (part + 1))
+            for c in range(S_CHUNKS):
+                nc.sync.dma_start(out=bw0[part][:, c, :, :], in_=bw0_in[:, c, :, half])
+
         for piece in range(2):
             cols = slice(S_HID // 2 * piece, S_HID // 2 * (piece + 1))
             nc.sync.dma_start(out=h2s[0][:, cols], in_=h2[half_rows(0), cols])
-        load_w0_half(0)
         nc.sync.dma_start(out=h2s[1][:], in_=h2[half_rows(1), 0:S_HID])
+        load_w0_half(0)
         load_w0_half(1)
         for h in range(HALVES):
             nc.sync.dma_start(out=fv[h][:], in_=features[half_rows(h), S_BYP:])
-        nc.sync.dma_start(out=bw1[0][:], in_=byp_W1.rearrange("(c q e) o -> q c e o", q=P, e=2))
         for h in range(HALVES):
             nc.sync.dma_start(out=fs[h][:], in_=features[half_rows(h), 0:S_BYP])
+        nc.sync.dma_start(out=bw1[0][:], in_=byp_W1.rearrange("(c q e) o -> q c e o", q=P, e=2))
         for h in range(HALVES):
             nc.sync.dma_start(out=h2v[h][:], in_=h2[half_rows(h), S_HID:])
+        nc.sync.dma_start(out=norm_rows[0:GAINS, :], in_=bn_weight.rearrange("(r c) -> r c", c=P))
+        nc.sync.dma_start(
+            out=norm_rows[GAINS : GAINS + S_TILES, :], in_=bn_bias.rearrange("(r c) -> r c", c=P)
+        )
+        load_bw0_half(0)
         load_scale_rows(nc, w1["planes"][0], lin3_W1_scales)
         nc.sync.dma_start(
             out=w1["words"][0][:].bitcast(I32),
             in_=lin3_W1_words.rearrange("g p b -> p g b").bitcast(I32),
         )
-        nc.sync.dma_start(out=norm_rows[0:GAINS, :], in_=bn_weight.rearrange("(r c) -> r c", c=P))
-        nc.sync.dma_start(
-            out=norm_rows[GAINS : GAINS + S_TILES, :], in_=bn_bias.rearrange("(r c) -> r c", c=P)
-        )
-        bw0_in = byp_W0.rearrange("(c q e) o -> q c e o", q=P, e=2)
-        for part in range(2):
-            half = slice(S_OUT // 2 * part, S_OUT // 2 * (part + 1))
-            for c in range(S_CHUNKS):
-                nc.sync.dma_start(out=bw0[part][:, c, :, :], in_=bw0_in[:, c, :, half])
+        load_bw0_half(1)
 
         s_grouped = [keep.tile([P, S_PASSES, P, 4], BF16, name="s_grouped%d" % h, align_bytes=64) for h in range(HALVES)]
         s_moving = [
@@ -281,20 +285,21 @@ def tile_feedforward_pb_kernel(
         idle_products(3)
         transpose_h2_scalars(0)
         quantise_h2_scalars(0)
-        idle_products(3)
-        scalar_mx_groups(range(0, S_TILES // 2), 0)
+        idle_products(2)
         transpose_h2_scalars(1)
         quantise_h2_scalars(1)
-        scalar_mx_groups(range(S_TILES // 2, S_TILES), 0)
+        idle_products(3)
         for h in range(HALVES):
-            sort_feature_vectors(h)
-        scalar_mx_groups(range(0, S_TILES - 2), 1)
+            scalar_mx_groups(range(0, S_TILES // 2), h)
         park_scalars(0)
         park_scalars(1)
+        for h in range(HALVES):
+            sort_feature_vectors(h)
+        for h in range(HALVES):
+            scalar_mx_groups(range(S_TILES // 2, S_TILES), h)
         for c in range(V_CHUNKS):
             transpose_feature_vectors(c, [c], range(BANK // P), v_feat_wide[:, c : c + 1, :, :])
         transpose_feature_vectors(V_CHUNKS, range(V_CHUNKS), range(BANK // P, V_COLS // P), v_feat_rest[:])
-        scalar_mx_groups(range(S_TILES - 2, S_TILES), 1)
         for pair in range(S_CHUNKS // 2):
             transpose_feature_scalars(pair)
         park_scalars(2)

@@ -31,8 +31,9 @@ BANK = 512
 GAINS = S_TILES + V_TILES
 EPS = 1e-5
 
+NORM_LAG, STORE_LAG = 2, 4
+WORK_BUFS = STORE_LAG + 2
 ROWS_BUFS = 12
-WORK_BUFS = 6
 
 FLOPS = 2 * NODES * (S_HID * S_OUT + DV * V_HID * V_OUT + S_BYP * S_OUT + DV * V_BYP * V_OUT)
 
@@ -429,19 +430,19 @@ def tile_feedforward_pb_kernel(
             )
             tile["inverse"] = inverse
 
-        def center(tile):
-            unit = work.tile([P, S_COLS], F32, tag="unit")
+        def weigh(m, tile):
+            weighed = work.tile([P, S_COLS], F32, tag="weighed")
             nc.vector.tensor_scalar(
-                out=unit[:], in0=tile["y"][:], scalar1=tile["minus_mean"][:], scalar2=tile["inverse"][:],
+                out=weighed[:], in0=tile["y"][:], scalar1=tile["minus_mean"][:], scalar2=norm_cols[:, m : m + 1],
                 op0=ALU.add, op1=ALU.mult,
             )
-            tile["unit"] = unit
+            tile["weighed"] = weighed
 
         def norm(kind, m, tile):
             if kind == "s":
                 z = work.tile([P, S_COLS], F32, tag="z")
                 nc.vector.tensor_scalar(
-                    out=z[:], in0=tile["unit"][:], scalar1=norm_cols[:, m : m + 1],
+                    out=z[:], in0=tile["weighed"][:], scalar1=tile["inverse"][:],
                     scalar2=norm_cols[:, GAINS + m : GAINS + m + 1], op0=ALU.mult, op1=ALU.add,
                 )
             else:
@@ -461,26 +462,27 @@ def tile_feedforward_pb_kernel(
                 banks.append(bank)
             return banks
 
-        def store_vector_half(m, h, bank, copy):
-            rows = work.tile([P, P, DV], F32, tag="rows", bufs=ROWS_BUFS)
-            copy(out=rows[:], in_=bank[:, 0:DV, :].rearrange("n d o -> n o d"))
-            first = S_OUT + DV * P * m
-            nc.sync.dma_start(
-                out=out[half_rows(h), first : first + DV * P], in_=rows[:].rearrange("n o d -> n (o d)")
-            )
+        def store_vector_tile(m, banks):
+            for h in range(HALVES):
+                rows = work.tile([P, P, DV], F32, tag="rows", bufs=ROWS_BUFS)
+                nc.scalar.copy(out=rows[:], in_=banks[h][:, 0:DV, :].rearrange("n d o -> n o d"))
+                first = S_OUT + DV * P * m
+                nc.sync.dma_start(
+                    out=out[half_rows(h), first : first + DV * P], in_=rows[:].rearrange("n o d -> n (o d)")
+                )
 
-        def transpose_scalar_tiles(zs):
-            bank = psum.tile([P, HALVES, len(zs), P], F32, tag="tr", name="s_rows_bank")
-            for i in range(len(zs)):
+        def transpose_scalar_pair(zs):
+            bank = psum.tile([P, HALVES, 2, P], F32, tag="tr", name="s_rows_bank")
+            for i in range(2):
                 for h in range(HALVES):
                     nc.tensor.transpose(bank[:, h, i, :], zs[i][:, block(h)], identity[:])
             return bank
 
-        def store_scalar_tiles(m, count, bank):
-            rows = work.tile([P, HALVES, count, P], F32, tag="rows", bufs=ROWS_BUFS)
-            nc.scalar.copy(out=rows[:], in_=bank[:])
+        def store_scalar_pair(m, bank):
+            rows = work.tile([P, HALVES, 2, P], F32, tag="rows", bufs=ROWS_BUFS)
+            nc.vector.tensor_copy(out=rows[:], in_=bank[:])
             nc.sync.dma_start(
-                out=out.rearrange("(h n) c -> n h c", n=P)[:, :, P * m : P * (m + count)],
+                out=out.rearrange("(h n) c -> n h c", n=P)[:, :, P * m : P * (m + 2)],
                 in_=rows[:].rearrange("n h m o -> n h (m o)"),
             )
 
@@ -488,46 +490,26 @@ def tile_feedforward_pb_kernel(
         for m in range(1, V_TILES):
             order.extend([("v", m), ("s", 2 * m), ("s", 2 * m + 1)])
         tiles = {}
-        banks = {}
-
-        def transpose_group(j):
-            banks["v"] = transpose_vector_tile(j, tiles["v", j]["z"])
-            banks["s"] = transpose_scalar_tiles([tiles["s", 2 * j]["z"], tiles["s", 2 * j + 1]["z"]])
-
-        def store_group(j):
-            for h in range(HALVES):
-                store_vector_half(j, h, banks["v"][h], nc.scalar.copy)
-            store_scalar_tiles(2 * j, 2, banks["s"])
-
-        for i in range(len(order)):
-            kind, m = order[i]
-            place = i % 3
-            before = order[i - 1] if i > 0 else None
-            norm_early = place == 2 and before[0] == "s"
-            if norm_early:
-                center(tiles[before])
-            tiles[kind, m] = scalar_product(m) if kind == "s" else vector_product(m)
-            if norm_early:
-                norm(*before, tiles[before])
-            elif i > 0 and before[0] == "s":
-                center(tiles[before])
+        for t in range(len(order) + STORE_LAG):
+            kind, m = order[t] if t < len(order) else (None, None)
+            if kind == "v":
+                tiles[kind, m] = vector_product(m)
             if kind == "s":
+                tiles[kind, m] = scalar_product(m)
                 negate_mean(tiles[kind, m])
-            stores = place == 1 and i > 3
-            if stores:
-                transpose_group(i // 3 - 1)
-            inverse_deviation(kind, tiles[kind, m])
-            if stores:
-                store_group(i // 3 - 1)
-            if i > 0 and not norm_early:
-                norm(*before, tiles[before])
-        last = V_TILES - 1
-        v_banks = transpose_vector_tile(last, tiles["v", last]["z"])
-        s_bank = transpose_scalar_tiles([tiles["s", 2 * last]["z"]])
-        store_vector_half(last, 0, v_banks[0], nc.vector.tensor_copy)
-        store_vector_half(last, 1, v_banks[1], nc.scalar.copy)
-        store_scalar_tiles(2 * last, 1, s_bank)
-        center(tiles[order[-1]])
-        norm(*order[-1], tiles[order[-1]])
-        s_bank = transpose_scalar_tiles([tiles["s", 2 * last + 1]["z"]])
-        store_scalar_tiles(2 * last + 1, 1, s_bank)
+            if 0 <= t - NORM_LAG < len(order):
+                normed = order[t - NORM_LAG]
+                norm(*normed, tiles[normed])
+            if kind == "s":
+                weigh(m, tiles[kind, m])
+            done_kind, done = order[t - STORE_LAG] if t >= STORE_LAG else (None, None)
+            if done_kind == "v":
+                banks = transpose_vector_tile(done, tiles["v", done]["z"])
+            elif done_kind == "s" and done % 2 == 1:
+                bank = transpose_scalar_pair([tiles["s", done - 1]["z"], tiles["s", done]["z"]])
+            if kind is not None:
+                inverse_deviation(kind, tiles[kind, m])
+            if done_kind == "v":
+                store_vector_tile(done, banks)
+            elif done_kind == "s" and done % 2 == 1:
+                store_scalar_pair(done - 1, bank)

@@ -31,8 +31,8 @@ BANK = 512
 GAINS = S_TILES + V_TILES
 EPS = 1e-5
 
-NORM_LAG, STORE_LAG = 2, 4
-WORK_BUFS = STORE_LAG + 2
+NORM_LAG, STORE_LAG = 2, {"v": 4, "s": 3}
+WORK_BUFS = 7
 ROWS_BUFS = 12
 
 FLOPS = 2 * NODES * (S_HID * S_OUT + DV * V_HID * V_OUT + S_BYP * S_OUT + DV * V_BYP * V_OUT)
@@ -286,7 +286,7 @@ def tile_feedforward_pb_kernel(
         idle_products(3)
         transpose_h2_scalars(0)
         quantise_h2_scalars(0)
-        idle_products(2)
+        idle_products(3)
         transpose_h2_scalars(1)
         quantise_h2_scalars(1)
         idle_products(3)
@@ -296,11 +296,12 @@ def tile_feedforward_pb_kernel(
         park_scalars(1)
         for h in range(HALVES):
             sort_feature_vectors(h)
-        for h in range(HALVES):
-            scalar_mx_groups(range(S_TILES // 2, S_TILES), h)
+        scalar_mx_groups(range(S_TILES // 2, S_TILES), 0)
+        scalar_mx_groups(range(S_TILES // 2, S_TILES - 1), 1)
         for c in range(V_CHUNKS):
             transpose_feature_vectors(c, [c], range(BANK // P), v_feat_wide[:, c : c + 1, :, :])
         transpose_feature_vectors(V_CHUNKS, range(V_CHUNKS), range(BANK // P, V_COLS // P), v_feat_rest[:])
+        scalar_mx_groups(range(S_TILES - 1, S_TILES), 1)
         for pair in range(S_CHUNKS // 2):
             transpose_feature_scalars(pair)
         park_scalars(2)
@@ -418,7 +419,7 @@ def tile_feedforward_pb_kernel(
 
         def inverse_deviation(kind, tile):
             cols = S_COLS if kind == "s" else V_COLS
-            squares = work.tile([P, cols], F32, tag="squares")
+            squares = work.tile([P, cols], F32, tag="squares", bufs=2)
             sum_of_squares = small.tile([P, 1], F32)
             nc.scalar.activation(
                 out=squares[:], in_=tile["y"][:], func=ACT.Square,
@@ -453,7 +454,7 @@ def tile_feedforward_pb_kernel(
                 )
             tile["z"] = z
 
-        def transpose_vector_tile(m, z):
+        def transpose_vector_tile(z):
             banks = []
             for h in range(HALVES):
                 bank = psum.tile([P, 4, P], F32, tag="tr", name="v_rows_bank")
@@ -465,7 +466,7 @@ def tile_feedforward_pb_kernel(
         def store_vector_tile(m, banks):
             for h in range(HALVES):
                 rows = work.tile([P, P, DV], F32, tag="rows", bufs=ROWS_BUFS)
-                nc.scalar.copy(out=rows[:], in_=banks[h][:, 0:DV, :].rearrange("n d o -> n o d"))
+                copy_words(nc, h, out=rows[:], in_=banks[h][:, 0:DV, :].rearrange("n d o -> n o d"))
                 first = S_OUT + DV * P * m
                 nc.sync.dma_start(
                     out=out[half_rows(h), first : first + DV * P], in_=rows[:].rearrange("n o d -> n (o d)")
@@ -480,17 +481,18 @@ def tile_feedforward_pb_kernel(
 
         def store_scalar_pair(m, bank):
             rows = work.tile([P, HALVES, 2, P], F32, tag="rows", bufs=ROWS_BUFS)
-            nc.vector.tensor_copy(out=rows[:], in_=bank[:])
+            nc.scalar.copy(out=rows[:], in_=bank[:])
             nc.sync.dma_start(
                 out=out.rearrange("(h n) c -> n h c", n=P)[:, :, P * m : P * (m + 2)],
                 in_=rows[:].rearrange("n h m o -> n h (m o)"),
             )
 
-        order = [("s", 0), ("v", 0), ("s", 1)]
-        for m in range(1, V_TILES):
-            order.extend([("v", m), ("s", 2 * m), ("s", 2 * m + 1)])
+        order = []
+        for m in range(V_TILES):
+            order.extend([("s", m), ("v", m)])
+        order.extend([("s", m) for m in range(V_TILES, S_TILES)])
         tiles = {}
-        for t in range(len(order) + STORE_LAG):
+        for t in range(len(order) + STORE_LAG["s"]):
             kind, m = order[t] if t < len(order) else (None, None)
             if kind == "v":
                 tiles[kind, m] = vector_product(m)
@@ -502,14 +504,22 @@ def tile_feedforward_pb_kernel(
                 norm(*normed, tiles[normed])
             if kind == "s":
                 weigh(m, tiles[kind, m])
-            done_kind, done = order[t - STORE_LAG] if t >= STORE_LAG else (None, None)
-            if done_kind == "v":
-                banks = transpose_vector_tile(done, tiles["v", done]["z"])
-            elif done_kind == "s" and done % 2 == 1:
-                bank = transpose_scalar_pair([tiles["s", done - 1]["z"], tiles["s", done]["z"]])
+            ready = [
+                (k, i)
+                for k in ("v", "s")
+                for (kk, i) in order[max(0, t - STORE_LAG[k]) : max(0, t - STORE_LAG[k] + 1)]
+                if kk == k and (k == "v" or i % 2 == 1)
+            ]
+            banks = [
+                transpose_vector_tile(tiles["v", i]["z"])
+                if k == "v"
+                else transpose_scalar_pair([tiles["s", i - 1]["z"], tiles["s", i]["z"]])
+                for (k, i) in ready
+            ]
             if kind is not None:
                 inverse_deviation(kind, tiles[kind, m])
-            if done_kind == "v":
-                store_vector_tile(done, banks)
-            elif done_kind == "s" and done % 2 == 1:
-                store_scalar_pair(done - 1, bank)
+            for (k, i), bank in zip(ready, banks):
+                if k == "v":
+                    store_vector_tile(i, bank)
+                else:
+                    store_scalar_pair(i - 1, bank)

@@ -150,10 +150,10 @@ def tile_feedforward_pb_kernel(
         identity = keep.tile([P, P], F32)
         make_identity(nc, identity[:])
 
-        def idle_products(count):
-            bank = psum.tile([P, BANK], F32, tag="tr", name="idle_bank")
+        def idle_products(count, moving):
+            bank = psum.tile([P, BANK], F32, tag="acc", name="idle_bank")
             for i in range(count):
-                nc.tensor.matmul(out=bank[:], lhsT=zeros[:, 0:P], rhs=zeros[:], start=True, stop=True)
+                nc.tensor.matmul(out=bank[:], lhsT=zeros[:, 0:P], rhs=moving, start=True, stop=True)
 
         w0_in = lin3_W0_words.rearrange("g p b -> p g b")
 
@@ -170,19 +170,19 @@ def tile_feedforward_pb_kernel(
             for c in range(S_CHUNKS):
                 nc.sync.dma_start(out=bw0[part][:, c, :, :], in_=bw0_in[:, c, :, half])
 
-        for piece in range(2):
-            cols = slice(S_HID // 2 * piece, S_HID // 2 * (piece + 1))
-            nc.sync.dma_start(out=h2s[0][:, cols], in_=h2[half_rows(0), cols])
+        for h in range(HALVES):
+            nc.sync.dma_start(out=fv[h][:], in_=features[half_rows(h), S_BYP:])
+        nc.sync.dma_start(out=h2s[0][:], in_=h2[half_rows(0), 0:S_HID])
+        bw1_in = byp_W1.rearrange("(c q e) o -> q c e o", q=P, e=2)
+        for c in range(V_CHUNKS):
+            nc.sync.dma_start(out=bw1[0][:, c, :, :], in_=bw1_in[:, c, :, :])
         nc.sync.dma_start(out=h2s[1][:], in_=h2[half_rows(1), 0:S_HID])
         load_w0_half(0)
         load_w0_half(1)
         for h in range(HALVES):
-            nc.sync.dma_start(out=fv[h][:], in_=features[half_rows(h), S_BYP:])
+            nc.sync.dma_start(out=h2v[h][:], in_=h2[half_rows(h), S_HID:])
         for h in range(HALVES):
             nc.sync.dma_start(out=fs[h][:], in_=features[half_rows(h), 0:S_BYP])
-        nc.sync.dma_start(out=bw1[0][:], in_=byp_W1.rearrange("(c q e) o -> q c e o", q=P, e=2))
-        for h in range(HALVES):
-            nc.sync.dma_start(out=h2v[h][:], in_=h2[half_rows(h), S_HID:])
         nc.sync.dma_start(out=norm_rows[0:GAINS, :], in_=bn_weight.rearrange("(r c) -> r c", c=P))
         nc.sync.dma_start(
             out=norm_rows[GAINS : GAINS + S_TILES, :], in_=bn_bias.rearrange("(r c) -> r c", c=P)
@@ -226,21 +226,23 @@ def tile_feedforward_pb_kernel(
                 )
 
         s_parked = keep.tile([P, S_TILES, S_COLS], F32)
-        s_acc = [psum.tile([P, 2, S_COLS], F32, tag="acc", name="s_acc") for pair in range(S_TILES // 2)]
 
-        def scalar_mx_groups(tiles, h):
-            for m in tiles:
-                mx_group(nc, s_acc[m // 2][:, m % 2, block(h)], w0, s_moving[h], m, slice(0, P))
+        def scalar_mx_pair(pair):
+            acc = psum.tile([P, 2, S_COLS], F32, tag="acc", name="s_acc")
+            for i in range(2):
+                for h in range(HALVES):
+                    mx_group(nc, acc[:, i, block(h)], w0, s_moving[h], 2 * pair + i, slice(0, P))
+            return acc
 
-        def park_scalars(pair):
+        def park_scalars(pair, acc):
             dst = s_parked[:, 2 * pair : 2 * pair + 2, :]
             if pair % 2 == 0:
                 nc.vector.tensor_scalar(
-                    out=dst, in0=s_acc[pair][:], scalar1=1.0 / math.sqrt(S_HID), scalar2=None, op0=ALU.mult
+                    out=dst, in0=acc[:], scalar1=1.0 / math.sqrt(S_HID), scalar2=None, op0=ALU.mult
                 )
             else:
                 nc.scalar.activation(
-                    out=dst, in_=s_acc[pair][:], func=ACT.Copy, scale=1.0 / math.sqrt(S_HID)
+                    out=dst, in_=acc[:], func=ACT.Copy, scale=1.0 / math.sqrt(S_HID)
                 )
 
         s_feat = keep.tile([P, S_CHUNKS, S_COLS, 2], BF16)
@@ -269,43 +271,16 @@ def tile_feedforward_pb_kernel(
             nc.vector.tensor_copy(out=f_sorted[h][:, 0:2, :], in_=by_part[:, 0:2, :])
             nc.scalar.copy(out=f_sorted[h][:, 2, :], in_=by_part[:, 2, :])
 
-        def transpose_feature_vectors(turn, chunks, blocks, out):
-            bank = transpose_four(
-                nc,
-                psum,
-                identity,
-                [f_sorted[b // DV][:].bitcast(F32)[:, b % DV, block(c)] for c in chunks for b in blocks],
-            )
+        def transpose_feature_block(bank, place, c, b):
+            nc.tensor.transpose(bank[:, place, :], f_sorted[b // DV][:].bitcast(F32)[:, b % DV, block(c)], identity[:])
+
+        def copy_feature_vectors(turn, bank, out):
             copy_words(
                 nc,
                 turn,
                 out=out.rearrange("q c n e -> q (c n e)").bitcast(F32),
                 in_=bank[:].rearrange("q b n -> q (b n)"),
             )
-
-        idle_products(3)
-        transpose_h2_scalars(0)
-        quantise_h2_scalars(0)
-        idle_products(3)
-        transpose_h2_scalars(1)
-        quantise_h2_scalars(1)
-        idle_products(3)
-        for h in range(HALVES):
-            scalar_mx_groups(range(0, S_TILES // 2), h)
-        park_scalars(0)
-        park_scalars(1)
-        for h in range(HALVES):
-            sort_feature_vectors(h)
-        scalar_mx_groups(range(S_TILES // 2, S_TILES), 0)
-        scalar_mx_groups(range(S_TILES // 2, S_TILES - 1), 1)
-        for c in range(V_CHUNKS):
-            transpose_feature_vectors(c, [c], range(BANK // P), v_feat_wide[:, c : c + 1, :, :])
-        transpose_feature_vectors(V_CHUNKS, range(V_CHUNKS), range(BANK // P, V_COLS // P), v_feat_rest[:])
-        scalar_mx_groups(range(S_TILES - 1, S_TILES), 1)
-        for pair in range(S_CHUNKS // 2):
-            transpose_feature_scalars(pair)
-        park_scalars(2)
-        park_scalars(3)
 
         v_sorted = [keep.tile([P, DV, 2 * V_PASSES, 2 * P], BF16, name="v_sorted%d" % h) for h in range(HALVES)]
         def sort_h2_vectors(h):
@@ -358,10 +333,8 @@ def tile_feedforward_pb_kernel(
                     )
 
         v_parked = keep.tile([P, V_TILES, V_COLS], F32)
-        sort_h2_vectors(0)
-        for m in range(V_TILES):
-            if m >= HALVES:
-                quantise_h2_vectors(m - HALVES)
+
+        def bypass_vector_tile(m):
             wide = psum.tile([P, BANK], F32, tag="acc")
             bypass_group(nc, wide[:], bw1, v_feat_wide, m)
             rest = psum.tile([P, V_COLS - BANK], F32, tag="acc")
@@ -372,15 +345,49 @@ def tile_feedforward_pb_kernel(
             nc.vector.tensor_scalar(
                 out=v_parked[:, m, BANK:], in0=rest[:], scalar1=1.0 / math.sqrt(V_BYP), scalar2=None, op0=ALU.mult
             )
+
+        idle_products(3, zeros[:])
+        for h in range(HALVES):
+            sort_feature_vectors(h)
+        idle_products(2, fv[0][:, 0:BANK])
+        wide_banks = [psum.tile([P, 4, P], F32, tag="tr", name="f_wide") for c in range(V_CHUNKS)]
+        for c in range(V_CHUNKS):
+            for b in range(DV):
+                transpose_feature_block(wide_banks[c], b, c, b)
+        idle_products(2, zeros[:])
+        for c in range(V_CHUNKS):
+            transpose_feature_block(wide_banks[c], DV, c, DV)
+            copy_feature_vectors(c, wide_banks[c], v_feat_wide[:, c : c + 1, :, :])
+        rest_bank = psum.tile([P, 4, P], F32, tag="tr", name="f_rest")
+        for c in range(V_CHUNKS):
+            for i in range(2):
+                transpose_feature_block(rest_bank, 2 * c + i, c, BANK // P + i)
+        copy_feature_vectors(V_CHUNKS, rest_bank, v_feat_rest[:])
+        transpose_h2_scalars(0)
+        for m in range(V_TILES):
+            bypass_vector_tile(m)
+            if m < HALVES:
+                quantise_h2_scalars(m)
             if m == 0:
+                transpose_h2_scalars(1)
+        sort_h2_vectors(0)
+        for pair in range(S_TILES // 2):
+            acc = scalar_mx_pair(pair)
+            park_scalars(pair, acc)
+            if pair == 0:
                 sort_h2_vectors(1)
+            if pair == 2:
+                transpose_h2_vectors(0)
+            if pair == 3:
                 nc.vector.tensor_copy(out=norm_rows_f32[:], in_=norm_rows[:])
-            if 1 <= m <= HALVES:
-                transpose_h2_vectors(m - 1)
-            if m == HALVES:
-                norm_bank = psum.tile([P, 4, P], F32, tag="tr")
-                nc.tensor.transpose(norm_bank[:, 0, :], norm_rows_f32[:], identity[:])
-                nc.vector.tensor_copy(out=norm_cols[:], in_=norm_bank[:, 0, 0 : GAINS + S_TILES])
+                for chunks in range(S_CHUNKS // 2):
+                    transpose_feature_scalars(chunks)
+                quantise_h2_vectors(0)
+        transpose_h2_vectors(1)
+        norm_bank = psum.tile([P, 4, P], F32, tag="tr")
+        nc.tensor.transpose(norm_bank[:, 0, :], norm_rows_f32[:], identity[:])
+        nc.vector.tensor_copy(out=norm_cols[:], in_=norm_bank[:, 0, 0 : GAINS + S_TILES])
+        quantise_h2_vectors(1)
 
         def scalar_product(m):
             acc = psum.tile([P, S_COLS], F32, tag="acc")

@@ -204,8 +204,10 @@ def tile_feedforward_pb_kernel(
             for h in range(HALVES)
         ]
 
-        def transpose_h2_scalars(h):
-            words = h2s[h][:].bitcast(F32).rearrange("n (g q u) -> n g u q", q=P, u=2)
+        h2s_words = [h2s[h][:].bitcast(F32).rearrange("n (g q u) -> n g u q", q=P, u=2) for h in range(HALVES)]
+        h2s_sorted = keep.tile([P, S_PASSES, 2, P], F32)
+
+        def transpose_h2_scalars(h, words):
             for g0 in range(0, S_PASSES, 2):
                 bank = transpose_four(
                     nc, psum, identity, [words[:, g0 + i, u, :] for i in range(2) for u in range(2)]
@@ -363,13 +365,16 @@ def tile_feedforward_pb_kernel(
             for i in range(2):
                 transpose_feature_block(rest_bank, 2 * c + i, c, BANK // P + i)
         copy_feature_vectors(V_CHUNKS, rest_bank, v_feat_rest[:])
-        transpose_h2_scalars(0)
+        transpose_h2_scalars(0, h2s_words[0])
+        nc.vector.tensor_copy(out=h2s_sorted[:], in_=h2s_words[1])
         for m in range(V_TILES):
             bypass_vector_tile(m)
-            if m < HALVES:
-                quantise_h2_scalars(m)
             if m == 0:
-                transpose_h2_scalars(1)
+                quantise_h2_scalars(0)
+            if m == 1:
+                transpose_h2_scalars(1, h2s_sorted)
+            if m == 2:
+                quantise_h2_scalars(1)
         sort_h2_vectors(0)
         for pair in range(S_TILES // 2):
             acc = scalar_mx_pair(pair)
@@ -523,10 +528,10 @@ def tile_feedforward_pb_kernel(
                 else transpose_scalar_pair([tiles["s", i - 1]["z"], tiles["s", i]["z"]])
                 for (k, i) in ready
             ]
-            if kind is not None:
-                inverse_deviation(kind, tiles[kind, m])
             for (k, i), bank in zip(ready, banks):
                 if k == "v":
                     store_vector_tile(i, bank)
                 else:
                     store_scalar_pair(i - 1, bank)
+            if kind is not None:
+                inverse_deviation(kind, tiles[kind, m])

@@ -27,6 +27,7 @@ S_COLS, V_COLS = NODES, DV * NODES
 S_PASSES, V_PASSES = S_HID // K_PASS, V_HID // K_PASS
 S_CHUNKS, V_CHUNKS = S_BYP // (2 * P), V_BYP // (2 * P)
 S_TILES, V_TILES = S_OUT // P, V_OUT // P
+F_PIECE = DV * 2 * P
 BANK = 512
 GAINS = S_TILES + V_TILES
 EPS = 1e-5
@@ -82,19 +83,22 @@ def mx_group(nc, acc, weight, moving, m, cols):
         )
 
 
-def bypass_group(nc, acc, weights, moving, m):
+def bypass_passes(nc, acc, weights, moving, m, c):
     share = weights[0].shape[3]
     some, first = weights[P * m // share], P * m % share
-    chunks = some.shape[1]
-    for c in range(chunks):
-        for e in range(2):
-            nc.tensor.matmul(
-                out=acc,
-                lhsT=some[:, c, e, first : first + P],
-                rhs=moving[:, c, :, e],
-                start=(c == 0 and e == 0),
-                stop=(c == chunks - 1 and e == 1),
-            )
+    for e in range(2):
+        nc.tensor.matmul(
+            out=acc,
+            lhsT=some[:, c, e, first : first + P],
+            rhs=moving[:, c, :, e],
+            start=(c == 0 and e == 0),
+            stop=(c == some.shape[1] - 1 and e == 1),
+        )
+
+
+def bypass_group(nc, acc, weights, moving, m):
+    for c in range(weights[0].shape[1]):
+        bypass_passes(nc, acc, weights, moving, m, c)
 
 
 def tile_feedforward_pb_kernel(
@@ -170,13 +174,14 @@ def tile_feedforward_pb_kernel(
             for c in range(S_CHUNKS):
                 nc.sync.dma_start(out=bw0[part][:, c, :, :], in_=bw0_in[:, c, :, half])
 
-        for h in range(HALVES):
-            nc.sync.dma_start(out=fv[h][:], in_=features[half_rows(h), S_BYP:])
-        nc.sync.dma_start(out=h2s[0][:], in_=h2[half_rows(0), 0:S_HID])
         bw1_in = byp_W1.rearrange("(c q e) o -> q c e o", q=P, e=2)
         for c in range(V_CHUNKS):
+            piece = slice(F_PIECE * c, F_PIECE * (c + 1))
+            for h in range(HALVES):
+                nc.sync.dma_start(out=fv[h][:, piece], in_=features[half_rows(h), S_BYP:][:, piece])
             nc.sync.dma_start(out=bw1[0][:, c, :, :], in_=bw1_in[:, c, :, :])
-        nc.sync.dma_start(out=h2s[1][:], in_=h2[half_rows(1), 0:S_HID])
+        for h in range(HALVES):
+            nc.sync.dma_start(out=h2s[h][:], in_=h2[half_rows(h), 0:S_HID])
         load_w0_half(0)
         load_w0_half(1)
         for h in range(HALVES):
@@ -205,9 +210,13 @@ def tile_feedforward_pb_kernel(
         ]
 
         h2s_words = [h2s[h][:].bitcast(F32).rearrange("n (g q u) -> n g u q", q=P, u=2) for h in range(HALVES)]
-        h2s_sorted = keep.tile([P, S_PASSES, 2, P], F32)
+        h2s_sorted = [keep.tile([P, S_PASSES, 2, P], F32, name="h2s_sorted%d" % h) for h in range(HALVES)]
 
-        def transpose_h2_scalars(h, words):
+        def sort_h2_scalars(h):
+            nc.vector.tensor_copy(out=h2s_sorted[h][:], in_=h2s_words[h])
+
+        def transpose_h2_scalars(h):
+            words = h2s_sorted[h]
             for g0 in range(0, S_PASSES, 2):
                 bank = transpose_four(
                     nc, psum, identity, [words[:, g0 + i, u, :] for i in range(2) for u in range(2)]
@@ -264,25 +273,34 @@ def tile_feedforward_pb_kernel(
                 in_=bank[:].rearrange("q b n -> q (b n)"),
             )
 
-        f_sorted = [keep.tile([P, DV, V_BYP], BF16, name="f_sorted%d" % h) for h in range(HALVES)]
+        f_sorted = [
+            [keep.tile([P, DV, 2 * P], BF16, name="f_sorted%d_%d" % (h, c)) for c in range(V_CHUNKS)]
+            for h in range(HALVES)
+        ]
         v_feat_wide = keep.tile([P, V_CHUNKS, BANK, 2], BF16)
         v_feat_rest = keep.tile([P, V_CHUNKS, V_COLS - BANK, 2], BF16)
 
-        def sort_feature_vectors(h):
-            by_part = fv[h][:].rearrange("n (i d) -> n d i", d=DV)
-            nc.vector.tensor_copy(out=f_sorted[h][:, 0:2, :], in_=by_part[:, 0:2, :])
-            nc.scalar.copy(out=f_sorted[h][:, 2, :], in_=by_part[:, 2, :])
+        def sort_feature_vectors(h, c):
+            by_part = fv[h][:, F_PIECE * c : F_PIECE * (c + 1)].rearrange("n (i d) -> n d i", d=DV)
+            nc.vector.tensor_copy(out=f_sorted[h][c][:, 0:2, :], in_=by_part[:, 0:2, :])
+            nc.scalar.copy(out=f_sorted[h][c][:, 2, :], in_=by_part[:, 2, :])
 
-        def transpose_feature_block(bank, place, c, b):
-            nc.tensor.transpose(bank[:, place, :], f_sorted[b // DV][:].bitcast(F32)[:, b % DV, block(c)], identity[:])
-
-        def copy_feature_vectors(turn, bank, out):
-            copy_words(
-                nc,
-                turn,
-                out=out.rearrange("q c n e -> q (c n e)").bitcast(F32),
-                in_=bank[:].rearrange("q b n -> q (b n)"),
-            )
+        def transpose_feature_vectors(c, h):
+            bank = psum.tile([P, 4, P], F32, tag="tr", name="f_bank")
+            for d in range(DV):
+                nc.tensor.transpose(bank[:, d, :], f_sorted[h][c][:].bitcast(F32)[:, d, :], identity[:])
+            wide = max(0, BANK // P - DV * h)
+            for dst, first, last, at in (
+                (v_feat_wide, 0, min(DV, wide), P * DV * h),
+                (v_feat_rest, min(DV, wide), DV, 0),
+            ):
+                if last > first:
+                    copy_words(
+                        nc,
+                        h,
+                        out=dst[:, c, at : at + P * (last - first), :].rearrange("q n e -> q (n e)").bitcast(F32),
+                        in_=bank[:, first:last, :].rearrange("q b n -> q (b n)"),
+                    )
 
         v_sorted = [keep.tile([P, DV, 2 * V_PASSES, 2 * P], BF16, name="v_sorted%d" % h) for h in range(HALVES)]
         def sort_h2_vectors(h):
@@ -336,11 +354,18 @@ def tile_feedforward_pb_kernel(
 
         v_parked = keep.tile([P, V_TILES, V_COLS], F32)
 
-        def bypass_vector_tile(m):
+        def open_bypass_vector_tile(m):
             wide = psum.tile([P, BANK], F32, tag="acc")
-            bypass_group(nc, wide[:], bw1, v_feat_wide, m)
             rest = psum.tile([P, V_COLS - BANK], F32, tag="acc")
-            bypass_group(nc, rest[:], bw1, v_feat_rest, m)
+            return m, wide, rest
+
+        def multiply_bypass_vector_tile(tile, c):
+            m, wide, rest = tile
+            bypass_passes(nc, wide[:], bw1, v_feat_wide, m, c)
+            bypass_passes(nc, rest[:], bw1, v_feat_rest, m, c)
+
+        def park_bypass_vector_tile(tile):
+            m, wide, rest = tile
             nc.scalar.activation(
                 out=v_parked[:, m, 0:BANK], in_=wide[:], func=ACT.Copy, scale=1.0 / math.sqrt(V_BYP)
             )
@@ -349,32 +374,37 @@ def tile_feedforward_pb_kernel(
             )
 
         idle_products(3, zeros[:])
+        idle_products(3, fv[0][:, 0:BANK])
         for h in range(HALVES):
-            sort_feature_vectors(h)
-        idle_products(2, fv[0][:, 0:BANK])
-        wide_banks = [psum.tile([P, 4, P], F32, tag="tr", name="f_wide") for c in range(V_CHUNKS)]
-        for c in range(V_CHUNKS):
-            for b in range(DV):
-                transpose_feature_block(wide_banks[c], b, c, b)
+            sort_feature_vectors(h, 0)
+        for h in range(HALVES):
+            transpose_feature_vectors(0, h)
         idle_products(2, zeros[:])
+        for h in range(HALVES):
+            sort_feature_vectors(h, 1)
+        first, second = open_bypass_vector_tile(0), open_bypass_vector_tile(1)
+        multiply_bypass_vector_tile(first, 0)
+        for h in range(HALVES):
+            transpose_feature_vectors(1, h)
+        multiply_bypass_vector_tile(second, 0)
+        sort_h2_scalars(0)
+        multiply_bypass_vector_tile(first, 1)
+        park_bypass_vector_tile(first)
+        multiply_bypass_vector_tile(second, 1)
+        park_bypass_vector_tile(second)
+        transpose_h2_scalars(0)
+        sort_h2_scalars(1)
+        third = open_bypass_vector_tile(2)
         for c in range(V_CHUNKS):
-            transpose_feature_block(wide_banks[c], DV, c, DV)
-            copy_feature_vectors(c, wide_banks[c], v_feat_wide[:, c : c + 1, :, :])
-        rest_bank = psum.tile([P, 4, P], F32, tag="tr", name="f_rest")
+            multiply_bypass_vector_tile(third, c)
+        park_bypass_vector_tile(third)
+        quantise_h2_scalars(0)
+        transpose_h2_scalars(1)
+        quantise_h2_scalars(1)
+        fourth = open_bypass_vector_tile(3)
         for c in range(V_CHUNKS):
-            for i in range(2):
-                transpose_feature_block(rest_bank, 2 * c + i, c, BANK // P + i)
-        copy_feature_vectors(V_CHUNKS, rest_bank, v_feat_rest[:])
-        transpose_h2_scalars(0, h2s_words[0])
-        nc.vector.tensor_copy(out=h2s_sorted[:], in_=h2s_words[1])
-        for m in range(V_TILES):
-            bypass_vector_tile(m)
-            if m == 0:
-                quantise_h2_scalars(0)
-            if m == 1:
-                transpose_h2_scalars(1, h2s_sorted)
-            if m == 2:
-                quantise_h2_scalars(1)
+            multiply_bypass_vector_tile(fourth, c)
+        park_bypass_vector_tile(fourth)
         sort_h2_vectors(0)
         for pair in range(S_TILES // 2):
             acc = scalar_mx_pair(pair)

@@ -27,6 +27,7 @@ S_COLS, V_COLS = NODES, DV * NODES
 S_PASSES, V_PASSES = S_HID // K_PASS, V_HID // K_PASS
 S_CHUNKS, V_CHUNKS = S_BYP // (2 * P), V_BYP // (2 * P)
 S_TILES, V_TILES = S_OUT // P, V_OUT // P
+BW0_WIDTHS = (2 * P, 2 * P, 4 * P)
 F_PIECE = DV * 2 * P
 BANK = 512
 GAINS = S_TILES + V_TILES
@@ -84,8 +85,10 @@ def mx_group(nc, acc, weight, moving, m, cols):
 
 
 def bypass_passes(nc, acc, weights, moving, m, c):
-    share = weights[0].shape[3]
-    some, first = weights[P * m // share], P * m % share
+    first, i = P * m, 0
+    while first >= weights[i].shape[3]:
+        first, i = first - weights[i].shape[3], i + 1
+    some = weights[i]
     for e in range(2):
         nc.tensor.matmul(
             out=acc,
@@ -137,7 +140,7 @@ def tile_feedforward_pb_kernel(
             "planes": [keep.tile([P, V_PASSES, V_OUT], U8, name="w1_planes", align_bytes=64)],
             "passes": V_PASSES,
         }
-        bw0 = [keep.tile([P, S_CHUNKS, 2, S_OUT // 2], BF16, name="bw0_%d" % part) for part in range(2)]
+        bw0 = [keep.tile([P, S_CHUNKS, 2, width], BF16, name="bw0_%d" % i) for i, width in enumerate(BW0_WIDTHS)]
         bw1 = [keep.tile([P, V_CHUNKS, 2, V_OUT], BF16, name="bw1")]
 
         for plane in w0["planes"] + w1["planes"]:
@@ -169,10 +172,10 @@ def tile_feedforward_pb_kernel(
 
         bw0_in = byp_W0.rearrange("(c q e) o -> q c e o", q=P, e=2)
 
-        def load_bw0_half(part):
-            half = slice(S_OUT // 2 * part, S_OUT // 2 * (part + 1))
+        def load_bw0(i):
+            some = slice(sum(BW0_WIDTHS[:i]), sum(BW0_WIDTHS[: i + 1]))
             for c in range(S_CHUNKS):
-                nc.sync.dma_start(out=bw0[part][:, c, :, :], in_=bw0_in[:, c, :, half])
+                nc.sync.dma_start(out=bw0[i][:, c, :, :], in_=bw0_in[:, c, :, some])
 
         bw1_in = byp_W1.rearrange("(c q e) o -> q c e o", q=P, e=2)
         for c in range(V_CHUNKS):
@@ -183,22 +186,23 @@ def tile_feedforward_pb_kernel(
         for h in range(HALVES):
             nc.sync.dma_start(out=h2s[h][:], in_=h2[half_rows(h), 0:S_HID])
         load_w0_half(0)
+        nc.sync.dma_start(out=h2v[0][:], in_=h2[half_rows(0), S_HID:])
         load_w0_half(1)
-        for h in range(HALVES):
-            nc.sync.dma_start(out=h2v[h][:], in_=h2[half_rows(h), S_HID:])
+        nc.sync.dma_start(out=h2v[1][:], in_=h2[half_rows(1), S_HID:])
         for h in range(HALVES):
             nc.sync.dma_start(out=fs[h][:], in_=features[half_rows(h), 0:S_BYP])
         nc.sync.dma_start(out=norm_rows[0:GAINS, :], in_=bn_weight.rearrange("(r c) -> r c", c=P))
         nc.sync.dma_start(
             out=norm_rows[GAINS : GAINS + S_TILES, :], in_=bn_bias.rearrange("(r c) -> r c", c=P)
         )
-        load_bw0_half(0)
-        load_scale_rows(nc, w1["planes"][0], lin3_W1_scales)
+        load_bw0(0)
         nc.sync.dma_start(
             out=w1["words"][0][:].bitcast(I32),
             in_=lin3_W1_words.rearrange("g p b -> p g b").bitcast(I32),
         )
-        load_bw0_half(1)
+        load_scale_rows(nc, w1["planes"][0], lin3_W1_scales)
+        for i in range(1, len(BW0_WIDTHS)):
+            load_bw0(i)
 
         s_grouped = [keep.tile([P, S_PASSES, P, 4], BF16, name="s_grouped%d" % h, align_bytes=64) for h in range(HALVES)]
         s_moving = [
@@ -246,15 +250,9 @@ def tile_feedforward_pb_kernel(
             return acc
 
         def park_scalars(pair, acc):
-            dst = s_parked[:, 2 * pair : 2 * pair + 2, :]
-            if pair % 2 == 0:
-                nc.vector.tensor_scalar(
-                    out=dst, in0=acc[:], scalar1=1.0 / math.sqrt(S_HID), scalar2=None, op0=ALU.mult
-                )
-            else:
-                nc.scalar.activation(
-                    out=dst, in_=acc[:], func=ACT.Copy, scale=1.0 / math.sqrt(S_HID)
-                )
+            nc.scalar.activation(
+                out=s_parked[:, 2 * pair : 2 * pair + 2, :], in_=acc[:], func=ACT.Copy, scale=1.0 / math.sqrt(S_HID)
+            )
 
         s_feat = keep.tile([P, S_CHUNKS, S_COLS, 2], BF16)
 
@@ -339,7 +337,7 @@ def tile_feedforward_pb_kernel(
                     blocks, dst = [words[:, 2, j, :] for j in range(4)], v_grouped_last[h]
                 bank = transpose_four(nc, psum, identity, blocks)
                 copy_words(
-                    nc, turn + h, out=dst[:].bitcast(F32), in_=bank[:].rearrange("q (a u) n -> q a n u", u=2)
+                    nc, turn + 1, out=dst[:].bitcast(F32), in_=bank[:].rearrange("q (a u) n -> q a n u", u=2)
                 )
 
         def quantise_h2_vectors(h):
@@ -374,7 +372,7 @@ def tile_feedforward_pb_kernel(
             )
 
         idle_products(3, zeros[:])
-        idle_products(3, fv[0][:, 0:BANK])
+        idle_products(2, fv[0][:, 0:BANK])
         for h in range(HALVES):
             sort_feature_vectors(h, 0)
         for h in range(HALVES):
@@ -409,20 +407,19 @@ def tile_feedforward_pb_kernel(
         for pair in range(S_TILES // 2):
             acc = scalar_mx_pair(pair)
             park_scalars(pair, acc)
-            if pair == 0:
+            if pair == 1:
+                transpose_h2_vectors(0)
                 sort_h2_vectors(1)
             if pair == 2:
-                transpose_h2_vectors(0)
-            if pair == 3:
-                nc.vector.tensor_copy(out=norm_rows_f32[:], in_=norm_rows[:])
-                for chunks in range(S_CHUNKS // 2):
-                    transpose_feature_scalars(chunks)
                 quantise_h2_vectors(0)
+        nc.vector.tensor_copy(out=norm_rows_f32[:], in_=norm_rows[:])
+        for chunks in range(S_CHUNKS // 2):
+            transpose_feature_scalars(chunks)
         transpose_h2_vectors(1)
         norm_bank = psum.tile([P, 4, P], F32, tag="tr")
         nc.tensor.transpose(norm_bank[:, 0, :], norm_rows_f32[:], identity[:])
-        nc.vector.tensor_copy(out=norm_cols[:], in_=norm_bank[:, 0, 0 : GAINS + S_TILES])
         quantise_h2_vectors(1)
+        nc.vector.tensor_copy(out=norm_cols[:], in_=norm_bank[:, 0, 0 : GAINS + S_TILES])
 
         def scalar_product(m):
             acc = psum.tile([P, S_COLS], F32, tag="acc")
@@ -508,7 +505,7 @@ def tile_feedforward_pb_kernel(
         def store_vector_tile(m, banks):
             for h in range(HALVES):
                 rows = work.tile([P, P, DV], F32, tag="rows", bufs=ROWS_BUFS)
-                copy_words(nc, h, out=rows[:], in_=banks[h][:, 0:DV, :].rearrange("n d o -> n o d"))
+                copy_words(nc, h + 1, out=rows[:], in_=banks[h][:, 0:DV, :].rearrange("n d o -> n o d"))
                 first = S_OUT + DV * P * m
                 nc.sync.dma_start(
                     out=out[half_rows(h), first : first + DV * P], in_=rows[:].rearrange("n o d -> n (o d)")

from contextlib import ExitStack
import math

import concourse.mybir as mybir
from concourse.masks import make_identity

BF16 = mybir.dt.bfloat16
F32 = mybir.dt.float32
I32 = mybir.dt.int32
U8 = mybir.dt.uint8
U32 = mybir.dt.uint32
FP8X4 = mybir.dt.float8_e4m3fn_x4
FP4X4 = mybir.dt.float4_e2m1fn_x4
ACT = mybir.ActivationFunctionType
ALU = mybir.AluOpType

P = 128
NODES = 256
HALVES = NODES // P
DV = 3
K_PASS = 4 * P

S_HID, V_HID = 2048, 1024
S_BYP, V_BYP = 1024, 512
S_OUT, V_OUT = 1024, 512
S_COLS, V_COLS = NODES, DV * NODES
S_PASSES, V_PASSES = S_HID // K_PASS, V_HID // K_PASS
S_CHUNKS, V_CHUNKS = S_BYP // (2 * P), V_BYP // (2 * P)
S_TILES, V_TILES = S_OUT // P, V_OUT // P
BW0_WIDTHS = (2 * P, 2 * P, 4 * P)
F_PIECE = DV * 2 * P
BANK = 512
GAINS = S_TILES + V_TILES
EPS = 1e-5

NORM_LAG, STORE_LAG = 2, {"v": 4, "s": 3}
WORK_BUFS = 7
ROWS_BUFS = 12

FLOPS = 2 * NODES * (S_HID * S_OUT + DV * V_HID * V_OUT + S_BYP * S_OUT + DV * V_BYP * V_OUT)


def half_rows(h):
    return slice(P * h, P * (h + 1))


def block(b):
    return slice(P * b, P * (b + 1))


def load_scale_rows(nc, planes, scales):
    by_row = scales.rearrange("g q n -> q g n")
    for r in range(4):
        nc.sync.dma_start(out=planes[r:P:32].bitcast(I32), in_=by_row[r:16:4].bitcast(I32))


def transpose_four(nc, psum, identity, blocks):
    bank = psum.tile([P, 4, P], F32, tag="tr")
    for j in range(4):
        nc.tensor.transpose(bank[:, j, :], blocks[j], identity[:])
    return bank


def copy_words(nc, turn, out, in_):
    if turn % 2 == 0:
        nc.vector.tensor_copy(out=out, in_=in_)
    else:
        nc.scalar.copy(out=out, in_=in_)


def mx_group(nc, acc, weight, moving, m, cols):
    passes = weight["passes"]
    share = weight["planes"][0].shape[2]
    words, planes, first = weight["words"][P * m // share], weight["planes"][P * m // share], P * m % share
    for g in range(passes):
        nc.tensor.matmul_mx(
            out=acc,
            lhsT=words[:, g, 2 * first : 2 * (first + P)].bitcast(FP4X4),
            lhsT_scale=planes[:, g, first : first + P],
            rhs=moving["codes"][:, g, cols].bitcast(FP8X4),
            rhs_scale=moving["planes"][:, g, cols],
            start=(g == 0),
            stop=(g == passes - 1),
        )


def bypass_passes(nc, acc, weights, moving, m, c):
    first, i = P * m, 0
    while first >= weights[i].shape[3]:
        first, i = first - weights[i].shape[3], i + 1
    some = weights[i]
    for e in range(2):
        nc.tensor.matmul(
            out=acc,
            lhsT=some[:, c, e, first : first + P],
            rhs=moving[:, c, :, e],
            start=(c == 0 and e == 0),
            stop=(c == some.shape[1] - 1 and e == 1),
        )


def bypass_group(nc, acc, weights, moving, m):
    for c in range(weights[0].shape[1]):
        bypass_passes(nc, acc, weights, moving, m, c)


def tile_feedforward_pb_kernel(
    tc,
    h2,
    features,
    lin3_W0_words,
    lin3_W0_scales,
    lin3_W1_words,
    lin3_W1_scales,
    byp_W0,
    byp_W1,
    bn_weight,
    bn_bias,
    out,
):
    nc = tc.nc
    with ExitStack() as stack:
        keep = stack.enter_context(tc.tile_pool(name="keep", bufs=1))
        work = stack.enter_context(tc.tile_pool(name="work", bufs=WORK_BUFS))
        small = stack.enter_context(tc.tile_pool(name="small", bufs=WORK_BUFS))
        psum = stack.enter_context(tc.psum_pool(name="psum", bufs=4))
        stack.enter_context(tc.manual_schedule())

        h2s = [keep.tile([P, S_HID], BF16, name="h2s%d" % h) for h in range(HALVES)]
        h2v = [keep.tile([P, DV * V_HID], BF16, name="h2v%d" % h) for h in range(HALVES)]
        fs = [keep.tile([P, S_BYP], BF16, name="fs%d" % h) for h in range(HALVES)]
        fv = [keep.tile([P, DV * V_BYP], BF16, name="fv%d" % h) for h in range(HALVES)]
        w0 = {
            "words": [keep.tile([P, S_PASSES, S_OUT], U8, name="w0_words%d" % part, align_bytes=64) for part in range(2)],
            "planes": [keep.tile([P, S_PASSES, S_OUT // 2], U8, name="w0_planes%d" % part, align_bytes=64) for part in range(2)],
            "passes": S_PASSES,
        }
        w1 = {
            "words": [keep.tile([P, V_PASSES, 2 * V_OUT], U8, name="w1_words", align_bytes=64)],
            "planes": [keep.tile([P, V_PASSES, V_OUT], U8, name="w1_planes", align_bytes=64)],
            "passes": V_PASSES,
        }
        bw0 = [keep.tile([P, S_CHUNKS, 2, width], BF16, name="bw0_%d" % i) for i, width in enumerate(BW0_WIDTHS)]
        bw1 = [keep.tile([P, V_CHUNKS, 2, V_OUT], BF16, name="bw1")]

        for plane in w0["planes"] + w1["planes"]:
            nc.vector.memset(plane[:].bitcast(I32), 0)
        eps = keep.tile([P, 1], F32)
        nc.vector.memset(eps[:], EPS)
        norm_rows = keep.tile([P, P], BF16)
        nc.vector.memset(norm_rows[:], 0.0)
        warm = keep.tile([P, 1], F32)
        nc.scalar.activation(out=warm[:], in_=eps[:], func=ACT.Abs_reciprocal_sqrt)

        zeros = keep.tile([P, BANK], BF16)
        nc.gpsimd.memset(zeros[:], 0.0)
        identity = keep.tile([P, P], F32)
        make_identity(nc, identity[:])

        def idle_products(count, moving):
            bank = psum.tile([P, BANK], F32, tag="acc", name="idle_bank")
            for i in range(count):
                nc.tensor.matmul(out=bank[:], lhsT=zeros[:, 0:P], rhs=moving, start=True, stop=True)

        w0_in = lin3_W0_words.rearrange("g p b -> p g b")

        def load_w0_half(part):
            half = slice(S_OUT // 2 * part, S_OUT // 2 * (part + 1))
            load_scale_rows(nc, w0["planes"][part], lin3_W0_scales[:, :, half])
            half = slice(S_OUT * part, S_OUT * (part + 1))
            nc.sync.dma_start(out=w0["words"][part][:].bitcast(I32), in_=w0_in[:, :, half].bitcast(I32))

        bw0_in = byp_W0.rearrange("(c q e) o -> q c e o", q=P, e=2)

        def load_bw0(i):
            some = slice(sum(BW0_WIDTHS[:i]), sum(BW0_WIDTHS[: i + 1]))
            for c in range(S_CHUNKS):
                nc.sync.dma_start(out=bw0[i][:, c, :, :], in_=bw0_in[:, c, :, some])

        bw1_in = byp_W1.rearrange("(c q e) o -> q c e o", q=P, e=2)
        for c in range(V_CHUNKS):
            piece = slice(F_PIECE * c, F_PIECE * (c + 1))
            for h in range(HALVES):
                nc.sync.dma_start(out=fv[h][:, piece], in_=features[half_rows(h), S_BYP:][:, piece])
            nc.sync.dma_start(out=bw1[0][:, c, :, :], in_=bw1_in[:, c, :, :])
        for h in range(HALVES):
            nc.sync.dma_start(out=h2s[h][:], in_=h2[half_rows(h), 0:S_HID])
        load_w0_half(0)
        nc.sync.dma_start(out=h2v[0][:], in_=h2[half_rows(0), S_HID:])
        load_w0_half(1)
        nc.sync.dma_start(out=h2v[1][:], in_=h2[half_rows(1), S_HID:])
        for h in range(HALVES):
            nc.sync.dma_start(out=fs[h][:], in_=features[half_rows(h), 0:S_BYP])
        nc.sync.dma_start(out=norm_rows[0:GAINS, :], in_=bn_weight.rearrange("(r c) -> r c", c=P))
        nc.sync.dma_start(
            out=norm_rows[GAINS : GAINS + S_TILES, :], in_=bn_bias.rearrange("(r c) -> r c", c=P)
        )
        load_bw0(0)
        nc.sync.dma_start(
            out=w1["words"][0][:].bitcast(I32),
            in_=lin3_W1_words.rearrange("g p b -> p g b").bitcast(I32),
        )
        load_scale_rows(nc, w1["planes"][0], lin3_W1_scales)
        for i in range(1, len(BW0_WIDTHS)):
            load_bw0(i)

        s_grouped = [keep.tile([P, S_PASSES, P, 4], BF16, name="s_grouped%d" % h, align_bytes=64) for h in range(HALVES)]
        s_moving = [
            {
                "codes": keep.tile([P, S_PASSES, P], U32, name="s_codes%d" % h, align_bytes=64),
                "planes": keep.tile([P, S_PASSES, P], U8, name="s_planes%d" % h, align_bytes=64),
            }
            for h in range(HALVES)
        ]

        h2s_words = [h2s[h][:].bitcast(F32).rearrange("n (g q u) -> n g u q", q=P, u=2) for h in range(HALVES)]
        h2s_sorted = [keep.tile([P, S_PASSES, 2, P], F32, name="h2s_sorted%d" % h) for h in range(HALVES)]

        def sort_h2_scalars(h):
            nc.vector.tensor_copy(out=h2s_sorted[h][:], in_=h2s_words[h])

        def transpose_h2_scalars(h):
            words = h2s_sorted[h]
            for g0 in range(0, S_PASSES, 2):
                bank = transpose_four(
                    nc, psum, identity, [words[:, g0 + i, u, :] for i in range(2) for u in range(2)]
                )
                copy_words(
                    nc,
                    g0 // 2,
                    out=s_grouped[h][:].bitcast(F32)[:, g0 : g0 + 2, :, :],
                    in_=bank[:].rearrange("q (g u) n -> q g n u", u=2),
                )

        def quantise_h2_scalars(h):
            for g0 in range(0, S_PASSES, 2):
                nc.vector.quantize_mx(
                    out=s_moving[h]["codes"][:, g0 : g0 + 2, :].rearrange("q g n -> q (g n)").bitcast(FP8X4),
                    scales=s_moving[h]["planes"][:, g0 : g0 + 2, :].rearrange("q g n -> q (g n)"),
                    in_=s_grouped[h][:, g0 : g0 + 2, :, :].rearrange("q g n t -> q (g n t)"),
                )

        s_parked = keep.tile([P, S_TILES, S_COLS], F32)

        def scalar_mx_pair(pair):
            acc = psum.tile([P, 2, S_COLS], F32, tag="acc", name="s_acc")
            for i in range(2):
                for h in range(HALVES):
                    mx_group(nc, acc[:, i, block(h)], w0, s_moving[h], 2 * pair + i, slice(0, P))
            return acc

        def park_scalars(pair, acc):
            nc.scalar.activation(
                out=s_parked[:, 2 * pair : 2 * pair + 2, :], in_=acc[:], func=ACT.Copy, scale=1.0 / math.sqrt(S_HID)
            )

        s_feat = keep.tile([P, S_CHUNKS, S_COLS, 2], BF16)

        def transpose_feature_scalars(pair):
            chunks = slice(2 * pair, 2 * pair + 2)
            bank = transpose_four(
                nc,
                psum,
                identity,
                [fs[h][:].bitcast(F32)[:, block(c)] for c in range(2 * pair, 2 * pair + 2) for h in range(HALVES)],
            )
            copy_words(
                nc,
                pair,
                out=s_feat[:, chunks, :, :].rearrange("q c n e -> q (c n e)").bitcast(F32),
                in_=bank[:].rearrange("q b n -> q (b n)"),
            )

        f_sorted = [
            [keep.tile([P, DV, 2 * P], BF16, name="f_sorted%d_%d" % (h, c)) for c in range(V_CHUNKS)]
            for h in range(HALVES)
        ]
        v_feat_wide = keep.tile([P, V_CHUNKS, BANK, 2], BF16)
        v_feat_rest = keep.tile([P, V_CHUNKS, V_COLS - BANK, 2], BF16)

        def sort_feature_vectors(h, c):
            by_part = fv[h][:, F_PIECE * c : F_PIECE * (c + 1)].rearrange("n (i d) -> n d i", d=DV)
            nc.vector.tensor_copy(out=f_sorted[h][c][:, 0:2, :], in_=by_part[:, 0:2, :])
            nc.scalar.copy(out=f_sorted[h][c][:, 2, :], in_=by_part[:, 2, :])

        def transpose_feature_vectors(c, h):
            bank = psum.tile([P, 4, P], F32, tag="tr", name="f_bank")
            for d in range(DV):
                nc.tensor.transpose(bank[:, d, :], f_sorted[h][c][:].bitcast(F32)[:, d, :], identity[:])
            wide = max(0, BANK // P - DV * h)
            for dst, first, last, at in (
                (v_feat_wide, 0, min(DV, wide), P * DV * h),
                (v_feat_rest, min(DV, wide), DV, 0),
            ):
                if last > first:
                    copy_words(
                        nc,
                        h,
                        out=dst[:, c, at : at + P * (last - first), :].rearrange("q n e -> q (n e)").bitcast(F32),
                        in_=bank[:, first:last, :].rearrange("q b n -> q (b n)"),
                    )

        v_sorted = [keep.tile([P, DV, 2 * V_PASSES, 2 * P], BF16, name="v_sorted%d" % h) for h in range(HALVES)]
        def sort_h2_vectors(h):
            by_part = h2v[h][:].rearrange(
                "n (g q u e d) -> n d g u q e", g=V_PASSES, q=P, u=2, e=2, d=DV
            )
            for d in range(DV):
                for g in range(V_PASSES):
                    dst = v_sorted[h][:, d, 2 * g : 2 * g + 2, :].rearrange("n u (q e) -> n u q e", e=2)
                    if d < 2:
                        nc.vector.tensor_copy(out=dst, in_=by_part[:, d, g])
                    else:
                        nc.scalar.copy(out=dst, in_=by_part[:, d, g])

        norm_rows_f32 = keep.tile([P, P], F32)
        norm_cols = keep.tile([P, GAINS + S_TILES], F32)

        v_grouped = [
            [keep.tile([P, 2, P, 4], BF16, name="v_grouped%d_%d" % (h, g), align_bytes=64) for g in range(V_PASSES)]
            for h in range(HALVES)
        ]
        v_grouped_last = [
            keep.tile([P, V_PASSES, P, 4], BF16, name="v_grouped_last%d" % h, align_bytes=64) for h in range(HALVES)
        ]
        v_moving = {
            "codes": keep.tile([P, V_PASSES, V_COLS], U32, name="v_codes", align_bytes=64),
            "planes": keep.tile([P, V_PASSES, V_COLS], U8, name="v_planes", align_bytes=64),
        }

        def transpose_h2_vectors(h):
            words = v_sorted[h][:].bitcast(F32)
            for turn in range(DV):
                if turn < V_PASSES:
                    blocks, dst = [words[:, d, 2 * turn + u, :] for d in range(2) for u in range(2)], v_grouped[h][turn]
                else:
                    blocks, dst = [words[:, 2, j, :] for j in range(4)], v_grouped_last[h]
                bank = transpose_four(nc, psum, identity, blocks)
                copy_words(
                    nc, turn + 1, out=dst[:].bitcast(F32), in_=bank[:].rearrange("q (a u) n -> q a n u", u=2)
                )

        def quantise_h2_vectors(h):
            for g in range(V_PASSES):
                for first, src in (0, v_grouped[h][g][:]), (2, v_grouped_last[h][:, g : g + 1, :, :]):
                    cols = slice(P * (DV * h + first), P * (DV * h + first + src.shape[1]))
                    nc.vector.quantize_mx(
                        out=v_moving["codes"][:, g, cols].bitcast(FP8X4),
                        scales=v_moving["planes"][:, g, cols],
                        in_=src.rearrange("q a n t -> q (a n t)"),
                    )

        v_parked = keep.tile([P, V_TILES, V_COLS], F32)

        def open_bypass_vector_tile(m):
            wide = psum.tile([P, BANK], F32, tag="acc")
            rest = psum.tile([P, V_COLS - BANK], F32, tag="acc")
            return m, wide, rest

        def multiply_bypass_vector_tile(tile, c):
            m, wide, rest = tile
            bypass_passes(nc, wide[:], bw1, v_feat_wide, m, c)
            bypass_passes(nc, rest[:], bw1, v_feat_rest, m, c)

        def park_bypass_vector_tile(tile):
            m, wide, rest = tile
            nc.scalar.activation(
                out=v_parked[:, m, 0:BANK], in_=wide[:], func=ACT.Copy, scale=1.0 / math.sqrt(V_BYP)
            )
            nc.vector.tensor_scalar(
                out=v_parked[:, m, BANK:], in0=rest[:], scalar1=1.0 / math.sqrt(V_BYP), scalar2=None, op0=ALU.mult
            )

        idle_products(3, zeros[:])
        idle_products(2, fv[0][:, 0:BANK])
        for h in range(HALVES):
            sort_feature_vectors(h, 0)
        for h in range(HALVES):
            transpose_feature_vectors(0, h)
        idle_products(2, zeros[:])
        for h in range(HALVES):
            sort_feature_vectors(h, 1)
        first, second = open_bypass_vector_tile(0), open_bypass_vector_tile(1)
        multiply_bypass_vector_tile(first, 0)
        for h in range(HALVES):
            transpose_feature_vectors(1, h)
        multiply_bypass_vector_tile(second, 0)
        sort_h2_scalars(0)
        multiply_bypass_vector_tile(first, 1)
        park_bypass_vector_tile(first)
        multiply_bypass_vector_tile(second, 1)
        park_bypass_vector_tile(second)
        transpose_h2_scalars(0)
        sort_h2_scalars(1)
        third = open_bypass_vector_tile(2)
        for c in range(V_CHUNKS):
            multiply_bypass_vector_tile(third, c)
        park_bypass_vector_tile(third)
        quantise_h2_scalars(0)
        transpose_h2_scalars(1)
        quantise_h2_scalars(1)
        fourth = open_bypass_vector_tile(3)
        for c in range(V_CHUNKS):
            multiply_bypass_vector_tile(fourth, c)
        park_bypass_vector_tile(fourth)
        sort_h2_vectors(0)
        for pair in range(S_TILES // 2):
            acc = scalar_mx_pair(pair)
            park_scalars(pair, acc)
            if pair == 1:
                transpose_h2_vectors(0)
                sort_h2_vectors(1)
            if pair == 2:
                quantise_h2_vectors(0)
        nc.vector.tensor_copy(out=norm_rows_f32[:], in_=norm_rows[:])
        for chunks in range(S_CHUNKS // 2):
            transpose_feature_scalars(chunks)
        transpose_h2_vectors(1)
        norm_bank = psum.tile([P, 4, P], F32, tag="tr")
        nc.tensor.transpose(norm_bank[:, 0, :], norm_rows_f32[:], identity[:])
        quantise_h2_vectors(1)
        nc.vector.tensor_copy(out=norm_cols[:], in_=norm_bank[:, 0, 0 : GAINS + S_TILES])

        def scalar_product(m):
            acc = psum.tile([P, S_COLS], F32, tag="acc")
            bypass_group(nc, acc[:], bw0, s_feat, m)
            y = work.tile([P, S_COLS], F32, tag="y")
            total = small.tile([P, 1], F32)
            nc.vector.scalar_tensor_tensor(
                out=y[:], in0=acc[:], scalar=1.0 / math.sqrt(S_BYP), in1=s_parked[:, m, :],
                op0=ALU.mult, op1=ALU.add, accum_out=total[:],
            )
            return {"y": y, "total": total}

        def negate_mean(tile):
            minus_mean = small.tile([P, 1], F32)
            nc.vector.tensor_scalar(
                out=minus_mean[:], in0=tile["total"][:], scalar1=-1.0 / S_COLS, scalar2=None, op0=ALU.mult
            )
            tile["minus_mean"] = minus_mean

        def vector_product(m):
            wide = psum.tile([P, BANK], F32, tag="acc")
            mx_group(nc, wide[:], w1, v_moving, m, slice(0, BANK))
            rest = psum.tile([P, V_COLS - BANK], F32, tag="acc")
            for b in range(BANK // P, V_COLS // P):
                mx_group(nc, rest[:, P * b - BANK : P * (b + 1) - BANK], w1, v_moving, m, block(b))
            y = work.tile([P, V_COLS], F32, tag="y")
            nc.vector.scalar_tensor_tensor(
                out=y[:, 0:BANK], in0=wide[:], scalar=1.0 / math.sqrt(V_HID), in1=v_parked[:, m, 0:BANK],
                op0=ALU.mult, op1=ALU.add,
            )
            nc.vector.scalar_tensor_tensor(
                out=y[:, BANK:], in0=rest[:], scalar=1.0 / math.sqrt(V_HID), in1=v_parked[:, m, BANK:],
                op0=ALU.mult, op1=ALU.add,
            )
            return {"y": y}

        def inverse_deviation(kind, tile):
            cols = S_COLS if kind == "s" else V_COLS
            squares = work.tile([P, cols], F32, tag="squares", bufs=2)
            sum_of_squares = small.tile([P, 1], F32)
            nc.scalar.activation(
                out=squares[:], in_=tile["y"][:], func=ACT.Square,
                bias=tile["minus_mean"][:] if kind == "s" else 0.0, accum_out=sum_of_squares[:],
            )
            inverse = small.tile([P, 1], F32)
            nc.scalar.activation(
                out=inverse[:], in_=sum_of_squares[:], func=ACT.Abs_reciprocal_sqrt, bias=eps[:], scale=1.0 / cols
            )
            tile["inverse"] = inverse

        def weigh(m, tile):
            weighed = work.tile([P, S_COLS], F32, tag="weighed")
            nc.vector.tensor_scalar(
                out=weighed[:], in0=tile["y"][:], scalar1=tile["minus_mean"][:], scalar2=norm_cols[:, m : m + 1],
                op0=ALU.add, op1=ALU.mult,
            )
            tile["weighed"] = weighed

        def norm(kind, m, tile):
            if kind == "s":
                z = work.tile([P, S_COLS], F32, tag="z")
                nc.vector.tensor_scalar(
                    out=z[:], in0=tile["weighed"][:], scalar1=tile["inverse"][:],
                    scalar2=norm_cols[:, GAINS + m : GAINS + m + 1], op0=ALU.mult, op1=ALU.add,
                )
            else:
                z = work.tile([P, V_COLS], F32, tag="z")
                nc.vector.tensor_scalar(
                    out=z[:], in0=tile["y"][:], scalar1=tile["inverse"][:],
                    scalar2=norm_cols[:, S_TILES + m : S_TILES + m + 1], op0=ALU.mult, op1=ALU.mult,
                )
            tile["z"] = z

        def transpose_vector_tile(z):
            banks = []
            for h in range(HALVES):
                bank = psum.tile([P, 4, P], F32, tag="tr", name="v_rows_bank")
                for d in range(DV):
                    nc.tensor.transpose(bank[:, d, :], z[:, block(DV * h + d)], identity[:])
                banks.append(bank)
            return banks

        def store_vector_tile(m, banks):
            for h in range(HALVES):
                rows = work.tile([P, P, DV], F32, tag="rows", bufs=ROWS_BUFS)
                copy_words(nc, h + 1, out=rows[:], in_=banks[h][:, 0:DV, :].rearrange("n d o -> n o d"))
                first = S_OUT + DV * P * m
                nc.sync.dma_start(
                    out=out[half_rows(h), first : first + DV * P], in_=rows[:].rearrange("n o d -> n (o d)")
                )

        def transpose_scalar_pair(zs):
            bank = psum.tile([P, HALVES, 2, P], F32, tag="tr", name="s_rows_bank")
            for i in range(2):
                for h in range(HALVES):
                    nc.tensor.transpose(bank[:, h, i, :], zs[i][:, block(h)], identity[:])
            return bank

        def store_scalar_pair(m, bank):
            rows = work.tile([P, HALVES, 2, P], F32, tag="rows", bufs=ROWS_BUFS)
            nc.scalar.copy(out=rows[:], in_=bank[:])
            nc.sync.dma_start(
                out=out.rearrange("(h n) c -> n h c", n=P)[:, :, P * m : P * (m + 2)],
                in_=rows[:].rearrange("n h m o -> n h (m o)"),
            )

        order = []
        for m in range(V_TILES):
            order.extend([("s", m), ("v", m)])
        order.extend([("s", m) for m in range(V_TILES, S_TILES)])
        tiles = {}
        for t in range(len(order) + STORE_LAG["s"]):
            kind, m = order[t] if t < len(order) else (None, None)
            if kind == "v":
                tiles[kind, m] = vector_product(m)
            if kind == "s":
                tiles[kind, m] = scalar_product(m)
                negate_mean(tiles[kind, m])
            if 0 <= t - NORM_LAG < len(order):
                normed = order[t - NORM_LAG]
                norm(*normed, tiles[normed])
            if kind == "s":
                weigh(m, tiles[kind, m])
            ready = [
                (k, i)
                for k in ("v", "s")
                for (kk, i) in order[max(0, t - STORE_LAG[k]) : max(0, t - STORE_LAG[k] + 1)]
                if kk == k and (k == "v" or i % 2 == 1)
            ]
            banks = [
                transpose_vector_tile(tiles["v", i]["z"])
                if k == "v"
                else transpose_scalar_pair([tiles["s", i - 1]["z"], tiles["s", i]["z"]])
                for (k, i) in ready
            ]
            for (k, i), bank in zip(ready, banks):
                if k == "v":
                    store_vector_tile(i, bank)
                else:
                    store_scalar_pair(i - 1, bank)
            if kind is not None:
                inverse_deviation(kind, tiles[kind, m])
